import numpy as np
import ml_dtypes


def mxq(x, axis, fmt="e4m3"):
    dtype, down = {"e4m3": (ml_dtypes.float8_e4m3fn, 7), "e5m2": (ml_dtypes.float8_e5m2, 14)}[fmt]
    v = np.moveaxis(np.asarray(x, np.float32).astype(ml_dtypes.bfloat16).astype(np.float64), axis, -1)
    blocks = v.reshape(v.shape[:-1] + (-1, 32))
    amax = np.abs(blocks).max(-1, keepdims=True)
    byte = np.maximum(np.where(amax > 0, np.frexp(amax)[1] - 1 + 127, 0) - down, 1)
    scale = np.exp2(byte - 127.0)
    codes = (blocks / scale).astype(np.float32).astype(dtype).astype(np.float64)
    return np.moveaxis((codes * scale).reshape(v.shape), -1, axis)


WIDE = False


def mx_kscale(k):
    if not WIDE:
        return np.ones(k)
    levels = np.array([10, -10, 5, -5, 0])
    a = np.random.permutation(np.resize(levels, k // 512 * 4)).reshape(k // 512, 4)
    idx = np.arange(k)
    return np.exp2(a[idx // 512, idx % 128 // 32])


BF16 = ml_dtypes.bfloat16


def bf(x):
    return np.asarray(x, np.float32).astype(BF16)


def f64(x):
    return np.asarray(x).astype(np.float64)


E2M1 = np.array([0.0, 0.5, 1.0, 1.5, 2.0, 3.0, 4.0, 6.0, -0.0, -0.5, -1.0, -1.5, -2.0, -3.0, -4.0, -6.0])


def pack_weight(w, fmt):
    k, n = w.shape
    w = f64(bf(w)).reshape(k // 32, 32, n)
    amax = np.abs(w).max(1)
    if fmt == "e4m3":
        byte = np.frexp(amax)[1] - 1 + 127 - 7
    else:
        mant, ex = np.frexp(amax / 6.0)
        byte = np.where(mant > 0.5, ex, ex - 1) + 127
    byte = np.clip(np.where(amax > 0, byte, 1), 1, 254)
    scaled = (w * np.exp2(127.0 - byte)[:, None, :]).reshape(k, n).astype(np.float32)
    by_word = np.ascontiguousarray(scaled.reshape(k // 512, 128, 4, n).transpose(0, 1, 3, 2))
    if fmt == "e4m3":
        words = by_word.astype(ml_dtypes.float8_e4m3fn).view(np.uint8)
    else:
        c = by_word.astype(ml_dtypes.float4_e2m1fn).view(np.uint8) & 0xF
        words = c[..., 0::2] | (c[..., 1::2] << 4)
    return np.ascontiguousarray(words), np.ascontiguousarray(byte.astype(np.uint8).reshape(k // 512, 16, n))


def unpack_weight(words, scales, fmt):
    g, p, n, _ = words.shape
    if fmt == "e4m3":
        vals = np.ascontiguousarray(words).view(ml_dtypes.float8_e4m3fn).astype(np.float64)
    else:
        nib = np.empty((g, p, n, 4), np.uint8)
        nib[..., 0::2] = words & 0xF
        nib[..., 1::2] = words >> 4
        vals = E2M1[nib]
    vals = vals * np.repeat(np.exp2(scales.astype(np.float64) - 127.0), 8, axis=1)[..., None]
    return vals.transpose(0, 1, 3, 2).reshape(g * 512, n)


B, S, H, HEAD_DIM, ROPE_DIM, RATIO = 1, 256, 4096, 1024, 64, 32
ROPE_THETA = 10000.0
NEG = -1e9
FMT = "e4m3"


def rotate_half_interleaved(x):
    x1 = x[..., 0::2]
    x2 = x[..., 1::2]
    return np.stack([-x2, x1], axis=-1).reshape(x.shape)


def softmax(v, axis):
    e = np.exp(v - v.max(axis=axis, keepdims=True))
    return e / e.sum(axis=axis, keepdims=True)


def setup_inputs():
    s = mx_kscale(H)
    hidden_states = bf(np.random.standard_normal((B, S, H)) * s)
    w_kv_words, w_kv_scales = pack_weight(np.random.standard_normal((H, 2 * HEAD_DIM)) * 2.0 / np.sqrt(H) / s[:, None], FMT)
    w_gate_words, w_gate_scales = pack_weight(np.random.standard_normal((H, 2 * HEAD_DIM)) * 1.0 / np.sqrt(H) / s[:, None], FMT)
    position_bias = bf(np.random.standard_normal((2 * RATIO, HEAD_DIM)) * 0.5)
    return {"hidden_states": hidden_states,
            "w_kv_words": w_kv_words,
            "w_kv_scales": w_kv_scales,
            "w_gate_words": w_gate_words,
            "w_gate_scales": w_gate_scales,
            "position_bias": position_bias}


def reference(hidden_states, w_kv_words, w_kv_scales, w_gate_words, w_gate_scales, position_bias):
    d, r = HEAD_DIM, RATIO
    n = S // r
    hq = mxq(f64(hidden_states), 2, "e4m3")
    kv = hq @ unpack_weight(w_kv_words, w_kv_scales, FMT)
    gate = hq @ unpack_weight(w_gate_words, w_gate_scales, FMT)

    chunk_kv = kv[:, : n * r].reshape(B, n, r, 2 * d)
    chunk_gate = gate[:, : n * r].reshape(B, n, r, 2 * d)

    kv_lo, kv_hi = chunk_kv[..., :d], chunk_kv[..., d:]
    g_lo, g_hi = chunk_gate[..., :d], chunk_gate[..., d:]
    prev_kv = np.concatenate([np.zeros_like(kv_lo[:, :1]), kv_lo[:, :-1]], axis=1)
    prev_g = np.concatenate([np.full_like(g_lo[:, :1], NEG), g_lo[:, :-1]], axis=1)
    win_kv = np.concatenate([prev_kv, kv_hi], axis=2)
    win_g = np.concatenate([prev_g, g_hi], axis=2)

    w = softmax(win_g + f64(position_bias)[None, None], 2)
    pooled = np.sum(w * win_kv, axis=2)

    positions = np.arange(n, dtype=np.float64) * r
    inv_freq = 1.0 / (ROPE_THETA ** (np.arange(0, ROPE_DIM, 2, dtype=np.float64) / ROPE_DIM))
    freqs = positions[:, None] * inv_freq[None, :]
    cos = np.repeat(np.cos(freqs), 2, axis=-1)
    sin = np.repeat(np.sin(freqs), 2, axis=-1)

    nope, rope = pooled[..., :-ROPE_DIM], pooled[..., -ROPE_DIM:]
    rotated = rope * cos[None] + rotate_half_interleaved(rope) * sin[None]
    return np.concatenate([nope, rotated], axis=-1)

@@ -1,0 +1,375 @@
+from contextlib import ExitStack
+import math
+
+import concourse.mybir as mybir
+from concourse.masks import make_identity
+
+F32 = mybir.dt.float32
+BF16 = mybir.dt.bfloat16
+I32 = mybir.dt.int32
+U32 = mybir.dt.uint32
+U8 = mybir.dt.uint8
+FP8X4 = mybir.dt.float8_e4m3fn_x4
+ALU = mybir.AluOpType
+ACT = mybir.ActivationFunctionType
+AX = mybir.AxisListType
+
+FLOPS = 2 * 256 * 4096 * 4096
+
+P = 128
+GROUPS = 8
+TOK = 256
+GATE, KV = 0, 1
+LO, HI = 0, 1
+RNG_A, RNG_B = 0, 1
+TWO_PI_HI = 6.28125
+TWO_PI_LO = 2.0 * math.pi - TWO_PI_HI
+
+
+def tile_deepseekv4csacompressor_w_kernel(
+    tc, hidden_states, w_kv_words, w_kv_scales, w_gate_words, w_gate_scales, position_bias, out
+):
+    nc = tc.nc
+    words = (w_gate_words, w_kv_words)
+    scales = (w_gate_scales, w_kv_scales)
+    with ExitStack() as ctx:
+        const = ctx.enter_context(tc.tile_pool(name="const", bufs=1))
+        wpool = ctx.enter_context(tc.tile_pool(name="weights", bufs=1))
+        work = ctx.enter_context(tc.tile_pool(name="work", bufs=2))
+        psum = ctx.enter_context(tc.psum_pool(name="psum", bufs=1))
+
+        ident_f = const.tile([P, P], F32, name="ident_f")
+        make_identity(nc, ident_f[:])
+        ident_b = const.tile([P, P], BF16, name="ident_b")
+        make_identity(nc, ident_b[:])
+        planes = []
+        for w in range(2):
+            pl = const.tile([P, 2, 2048], U8, name="planes%d" % w, align_bytes=64)
+            nc.vector.memset(pl[:].bitcast(I32), 0)
+            planes.append(pl)
+        pooled_t = const.tile([P, P], F32, name="pooled_t")
+        nc.gpsimd.memset(pooled_t[:], 0.0)
+        freq = const.tile([P, 32], F32, name="freq")
+        nc.gpsimd.memset(freq[:, 0:1], 1.0)
+        row_i = const.tile([P, 1], I32, name="row_i")
+        nc.gpsimd.iota(row_i[:], pattern=[[0, 1]], base=0, channel_multiplier=1)
+
+        bias_sb = const.tile([P, 512], BF16, name="bias_sb")
+        nc.scalar.dma_start(out=bias_sb[:], in_=position_bias.rearrange("s (h c) -> (s h) c", h=2))
+        x_sb = {}
+        for half in range(2):
+            for tt in range(2):
+                xs = const.tile([P, 2048], BF16, name="x_sb%d_%d" % (tt, half))
+                nc.sync.dma_start(
+                    out=xs[:],
+                    in_=hidden_states[0, tt * P : (tt + 1) * P, half * 2048 : (half + 1) * 2048],
+                )
+                x_sb[(tt, half)] = xs
+
+        def load_scales(queue, view, w, a):
+            for q in range(4):
+                queue.dma_start(
+                    out=planes[w][32 * q : 32 * q + 16, a, :].bitcast(view),
+                    in_=scales[w][4 * a : 4 * a + 4, 4 * q : 4 * q + 4, :].bitcast(view),
+                )
+
+        def first_col(rng, half):
+            return 1024 * half + (512 if rng == RNG_A else 0)
+
+        wt = {}
+
+        def load_words(w, rng, half, group_lists):
+            c0 = first_col(rng, half)
+            for gs in group_lists:
+                t = wpool.tile(
+                    [P, len(gs), 512], U32, name="w%d_%d_%d_%d" % (w, rng, half, gs[0]), align_bytes=64
+                )
+                nc.sync.dma_start(
+                    out=t[:].bitcast(I32),
+                    in_=words[w][gs[0] : gs[-1] + 1, :, c0 : c0 + 512, :]
+                    .rearrange("g p n t -> p g (n t)")
+                    .bitcast(I32),
+                )
+                for k in range(len(gs)):
+                    wt[(w, rng, half, gs[k])] = t[:, k, :]
+
+        pairs = [[0, 1], [2, 3], [4, 5], [6, 7]]
+        load_scales(nc.sync, I32, GATE, 0)
+        load_words(GATE, RNG_A, HI, [[0], [1], [2, 3]])
+        load_scales(nc.sync, I32, GATE, 1)
+        load_words(GATE, RNG_A, HI, [[4, 5], [6, 7]])
+        load_scales(nc.gpsimd, F32, KV, 0)
+        load_scales(nc.gpsimd, F32, KV, 1)
+        load_words(GATE, RNG_A, LO, pairs)
+        load_words(GATE, RNG_B, HI, pairs)
+        load_words(GATE, RNG_B, LO, pairs)
+        load_words(KV, RNG_A, HI, pairs)
+        load_words(KV, RNG_A, LO, pairs)
+        load_words(KV, RNG_B, HI, pairs)
+        load_words(KV, RNG_B, LO, [[0, 1], [2, 3], [4, 5], [6], [7]])
+
+        grouped = []
+        x_codes = []
+        x_scl = []
+        for g in range(GROUPS):
+            grouped.append(const.tile([P, 4 * TOK], BF16, name="grouped%d" % g, align_bytes=64))
+            x_codes.append(const.tile([P, TOK], U32, name="x_codes%d" % g, align_bytes=64))
+            x_scl.append(const.tile([P, TOK], U8, name="x_scl%d" % g, align_bytes=64))
+
+        def quantise(g):
+            nc.vector.quantize_mx(
+                out=x_codes[g][:].bitcast(FP8X4), scales=x_scl[g][:], in_=grouped[g][:]
+            )
+
+        for g in range(GROUPS):
+            xt = psum.tile([P, 2, TOK], F32, tag="bank%d" % g, name="xt%d" % g)
+            for tt in range(2):
+                src = x_sb[(tt, g // 4)][:].bitcast(F32)
+                for u in range(2):
+                    lo_w = 256 * (g % 4)
+                    nc.tensor.transpose(
+                        xt[:, u, tt * P : (tt + 1) * P], src[:, lo_w + u : lo_w + 256 : 2], ident_f[:]
+                    )
+            dst = grouped[g][:].bitcast(F32).rearrange("p (t u) -> p t u", u=2)
+            if g % 4 == 3:
+                nc.vector.tensor_copy(out=dst, in_=xt[:].rearrange("p u t -> p t u"))
+            else:
+                nc.scalar.copy(out=dst, in_=xt[:].rearrange("p u t -> p t u"))
+            if g >= 1:
+                quantise(g - 1)
+        quantise(GROUPS - 1)
+
+        bt = psum.tile([P, 4, P], BF16, tag="bank7", name="bt")
+        for b in range(4):
+            nc.tensor.transpose(bt[:, b, :], bias_sb[:, b * P : (b + 1) * P], ident_b[:])
+        neg_bias = const.tile([P, 8, 64], F32, name="neg_bias")
+        bt_v = bt[:].rearrange("p b (s h) -> p h b s", h=2)
+        nb_v = neg_bias[:].rearrange("p (h b) s -> p h b s", h=2)
+        nc.vector.tensor_scalar(
+            out=nb_v[:, :, :, 0:32], in0=bt_v[:, :, :, 32:64], scalar1=-1.0, scalar2=None, op0=ALU.mult
+        )
+        nc.vector.tensor_scalar(
+            out=nb_v[:, :, :, 32:64], in0=bt_v[:, :, :, 0:32], scalar1=-1.0, scalar2=None, op0=ALU.mult
+        )
+
+        win_i = const.tile([P, 1], I32, name="win_i")
+        nc.vector.tensor_scalar(
+            out=win_i[:], in0=row_i[:], scalar1=2, scalar2=7, op0=ALU.logical_shift_right, op1=ALU.bitwise_and
+        )
+        unit_i = const.tile([P, 1], I32, name="unit_i")
+        nc.vector.tensor_single_scalar(out=unit_i[:], in_=row_i[:], scalar=3, op=ALU.bitwise_and)
+        win_f = const.tile([P, 1], F32, name="win_f")
+        nc.vector.tensor_copy(out=win_f[:], in_=win_i[:])
+        unit_f = const.tile([P, 1], F32, name="unit_f")
+        nc.vector.tensor_copy(out=unit_f[:], in_=unit_i[:])
+        step_f = const.tile([P, 1], F32, name="step_f")
+        nc.vector.tensor_scalar(
+            out=step_f[:], in0=unit_f[:], scalar1=3.0, scalar2=32.0, op0=ALU.is_equal, op1=ALU.mult
+        )
+        for b in range(5):
+            n = 2 ** b
+            nc.vector.tensor_scalar(
+                out=freq[:, n : 2 * n],
+                in0=freq[:, 0:n],
+                scalar1=10000.0 ** (-2.0 * n / 64.0),
+                scalar2=None,
+                op0=ALU.mult,
+            )
+        pos_f = const.tile([P, 1], F32, name="pos_f")
+        nc.vector.tensor_tensor(out=pos_f[:], in0=win_f[:], in1=step_f[:], op=ALU.mult)
+        angle = const.tile([P, 64], F32, name="angle")
+        nc.vector.tensor_scalar(
+            out=angle[:, 0:32], in0=freq[:], scalar1=pos_f[:, 0:1], scalar2=None, op0=ALU.mult
+        )
+        nc.vector.tensor_scalar(
+            out=angle[:, 32:64], in0=angle[:, 0:32], scalar1=0.5 * math.pi, scalar2=None, op0=ALU.add
+        )
+        turns_i = const.tile([P, 64], I32, name="turns_i")
+        nc.vector.tensor_scalar(
+            out=turns_i[:], in0=angle[:], scalar1=0.5 / math.pi, scalar2=None, op0=ALU.mult
+        )
+        turns_f = const.tile([P, 64], F32, name="turns_f")
+        nc.vector.tensor_copy(out=turns_f[:], in_=turns_i[:])
+        red = const.tile([P, 64], F32, name="red")
+        nc.vector.scalar_tensor_tensor(
+            out=red[:], in0=turns_f[:], scalar=-TWO_PI_HI, in1=angle[:], op0=ALU.mult, op1=ALU.add
+        )
+        nc.vector.scalar_tensor_tensor(
+            out=red[:], in0=turns_f[:], scalar=-TWO_PI_LO, in1=red[:], op0=ALU.mult, op1=ALU.add
+        )
+        fold = const.tile([P, 64], F32, name="fold")
+        nc.vector.tensor_scalar(
+            out=fold[:], in0=red[:], scalar1=math.pi, scalar2=-2.0 * math.pi, op0=ALU.is_gt, op1=ALU.mult
+        )
+        nc.vector.tensor_tensor(out=red[:], in0=red[:], in1=fold[:], op=ALU.add)
+        sin_cos = const.tile([P, 64], F32, name="sin_cos")
+        nc.scalar.activation(out=sin_cos[:], in_=red[:], func=ACT.Sin)
+
+        def mx_block(w, rng, half, outs):
+            c0 = first_col(rng, half)
+            for g in range(GROUPS):
+                for j in range(4):
+                    nc.tensor.matmul_mx(
+                        out=outs[j],
+                        lhsT=wt[(w, rng, half, g)][:, j * P : (j + 1) * P].bitcast(FP8X4),
+                        lhsT_scale=planes[w][4 * (g % 4) : P, g // 4, c0 + j * P : c0 + (j + 1) * P],
+                        rhs=x_codes[g][:].bitcast(FP8X4),
+                        rhs_scale=x_scl[g][:],
+                        start=(g == 0),
+                        stop=(g == GROUPS - 1),
+                    )
+
+        e_tiles = {}
+        neg_max = {}
+        sums = {}
+        rden = {}
+
+        def unit_of(rng, j):
+            return j + (4 if rng == RNG_A else 0)
+
+        def softmax_weights(rng, banks):
+            nm = const.tile([P, 4, 16], F32, name="neg_max%d" % rng)
+            sm = const.tile([P, 4, 16], F32, name="sums%d" % rng)
+            neg_max[rng] = nm
+            sums[rng] = sm
+            for j in range(4):
+                u = unit_of(rng, j)
+                e = const.tile([P, 512], F32, name="e%d" % u)
+                e_tiles[u] = e
+                nc.vector.tensor_tensor(
+                    out=e[:].rearrange("p (h k s) -> p h k s", h=2, k=8),
+                    in0=neg_bias[:, u, :]
+                    .rearrange("p (h s) -> p h s", h=2)
+                    .unsqueeze(2)
+                    .to_broadcast([P, 2, 8, 32]),
+                    in1=banks[j][:].rearrange("p (h k s) -> p h k s", h=2, k=8),
+                    op=ALU.subtract,
+                )
+                nc.vector.tensor_reduce(
+                    out=nm[:, j, 0:15],
+                    in_=e[:, 0:480].rearrange("p (k s) -> p k s", s=32),
+                    axis=AX.X,
+                    op=ALU.min,
+                )
+                nc.vector.tensor_tensor(
+                    out=nm[:, j, 1:8], in0=nm[:, j, 1:8], in1=nm[:, j, 8:15], op=ALU.min
+                )
+                for k in range(15):
+                    win = k if k < 8 else k - 7
+                    nc.scalar.activation(
+                        out=e[:, 32 * k : 32 * k + 32],
+                        in_=e[:, 32 * k : 32 * k + 32],
+                        func=ACT.Exp,
+                        bias=nm[:, j, win : win + 1],
+                        scale=-1.0,
+                        accum_out=sm[:, j, k : k + 1],
+                    )
+            den = const.tile([P, 4, 8], F32, name="den%d" % rng)
+            nc.vector.tensor_copy(out=den[:, :, 0:1], in_=sm[:, :, 0:1])
+            nc.vector.tensor_tensor(out=den[:, :, 1:8], in0=sm[:, :, 1:8], in1=sm[:, :, 8:15], op=ALU.add)
+            rd = const.tile([P, 4, 8], F32, name="rden%d" % rng)
+            nc.vector.reciprocal(out=rd[:], in_=den[:])
+            rden[rng] = rd
+
+        def finish(rng, num):
+            nc.vector.tensor_tensor(out=num[:, :, 1:8], in0=num[:, :, 1:8], in1=num[:, :, 8:15], op=ALU.add)
+            nc.vector.tensor_tensor(
+                out=pooled_t[:, 32 * rng : 32 * rng + 32].rearrange("p (i j) -> p j i", j=4),
+                in0=num[:, :, 0:8],
+                in1=rden[rng][:],
+                op=ALU.mult,
+            )
+
+        out_v = out[0].rearrange("i (h j c) -> h i j c", h=2, j=4)
+
+        for rng in (RNG_A, RNG_B):
+            banks = [
+                psum.tile([P, 512], F32, tag="bank%d" % (4 * rng + j), name="gate%d_%d" % (rng, j))
+                for j in range(4)
+            ]
+            mx_block(GATE, rng, HI, [b[:, 0:256] for b in banks])
+            mx_block(GATE, rng, LO, [b[:, 256:512] for b in banks])
+            softmax_weights(rng, banks)
+
+        for j in range(4):
+            e_lo = e_tiles[j][:, 256:480].rearrange("p (k s) -> p k s", s=32)
+            nc.vector.tensor_tensor(
+                out=e_lo,
+                in0=e_lo,
+                in1=rden[RNG_B][:, j, 1:8].unsqueeze(2).to_broadcast([P, 7, 32]),
+                op=ALU.mult,
+            )
+
+        banks = [psum.tile([P, 512], F32, tag="bank%d" % j, name="kv_a%d" % j) for j in range(4)]
+        mx_block(KV, RNG_A, HI, [b[:, 0:256] for b in banks])
+        mx_block(KV, RNG_A, LO, [b[:, 256:512] for b in banks])
+        prod = work.tile([P, 4, 512], F32, tag="prod", name="prod_a")
+        for j in range(4):
+            nc.vector.tensor_tensor(
+                out=prod[:, j, 0:480], in0=banks[j][:, 0:480], in1=e_tiles[4 + j][:, 0:480], op=ALU.mult
+            )
+        num_a = const.tile([P, 4, 16], F32, name="num_a")
+        nc.vector.tensor_reduce(
+            out=num_a[:, :, 0:15],
+            in_=prod[:, :, 0:480].rearrange("p j (k s) -> p j k s", s=32),
+            axis=AX.X,
+            op=ALU.add,
+        )
+        finish(RNG_A, num_a)
+
+        num_b = const.tile([P, 4, 16], F32, name="num_b")
+        banks = [psum.tile([P, 256], F32, tag="bank%d" % (4 + j), name="kv_bh%d" % j) for j in range(4)]
+        mx_block(KV, RNG_B, HI, [b[:] for b in banks])
+        prod = work.tile([P, 4, 512], F32, tag="prod", name="prod_bh")
+        for j in range(4):
+            nc.vector.tensor_tensor(
+                out=prod[:, j, 0:256], in0=banks[j][:], in1=e_tiles[j][:, 0:256], op=ALU.mult
+            )
+        nc.vector.tensor_reduce(
+            out=num_b[:, :, 0:8],
+            in_=prod[:, :, 0:256].rearrange("p j (k s) -> p j k s", s=32),
+            axis=AX.X,
+            op=ALU.add,
+        )
+        prod_bl = const.tile([P, 4, 7, 33], F32, name="prod_bl")
+        pooled_b = pooled_t[:, 32:64].rearrange("p (i j) -> p j i", j=4)
+        nc.vector.tensor_tensor(
+            out=prod_bl[:, :, :, 32], in0=num_b[:, :, 1:8], in1=rden[RNG_B][:, :, 1:8], op=ALU.mult
+        )
+        nc.vector.tensor_tensor(
+            out=pooled_b[:, :, 0], in0=num_b[:, :, 0], in1=rden[RNG_B][:, :, 0], op=ALU.mult
+        )
+
+        fa = psum.tile([P, P], F32, tag="bank4", name="fa")
+        nc.tensor.transpose(fa[:], pooled_t[:], ident_f[:])
+        res_a = const.tile([P, P], F32, name="res_a")
+        t_cos = const.tile([P, 32, 2], F32, name="t_cos")
+        t_sin = const.tile([P, 32, 2], F32, name="t_sin")
+        R = 32
+        v = fa[0:R, 64:128].rearrange("p (j e) -> p j e", e=2)
+        o = res_a[0:R, 64:128].rearrange("p (j e) -> p j e", e=2)
+        nc.vector.tensor_copy(out=res_a[0:R, 0:64], in_=fa[0:R, 0:64])
+        nc.vector.tensor_tensor(
+            out=t_cos[0:R], in0=v, in1=sin_cos[0:R, 32:64].unsqueeze(2).to_broadcast([R, 32, 2]), op=ALU.mult
+        )
+        nc.vector.tensor_tensor(out=t_sin[0:R, :, 0], in0=v[:, :, 1], in1=sin_cos[0:R, 0:32], op=ALU.mult)
+        nc.vector.tensor_tensor(out=t_sin[0:R, :, 1], in0=v[:, :, 0], in1=sin_cos[0:R, 0:32], op=ALU.mult)
+        nc.vector.tensor_tensor(out=o[:, :, 0], in0=t_cos[0:R, :, 0], in1=t_sin[0:R, :, 0], op=ALU.subtract)
+        nc.vector.tensor_tensor(out=o[:, :, 1], in0=t_cos[0:R, :, 1], in1=t_sin[0:R, :, 1], op=ALU.add)
+        nc.gpsimd.dma_start(out=out_v[1], in_=res_a[0:R, :])
+
+        banks = [psum.tile([P, 256], F32, tag="bank%d" % j, name="kv_bl%d" % j) for j in range(4)]
+        mx_block(KV, RNG_B, LO, [b[:] for b in banks])
+        for j in range(4):
+            nc.vector.tensor_tensor(
+                out=prod_bl[:, j, :, 0:32],
+                in0=banks[j][:, 0:224].rearrange("p (k s) -> p k s", s=32),
+                in1=e_tiles[j][:, 256:480].rearrange("p (k s) -> p k s", s=32),
+                op=ALU.mult,
+            )
+        nc.vector.tensor_reduce(out=pooled_b[:, :, 1:8], in_=prod_bl[:], axis=AX.X, op=ALU.add)
+        fb = psum.tile([P, P], F32, tag="bank5", name="fb")
+        nc.tensor.transpose(fb[:], pooled_t[:], ident_f[:])
+        res_b = const.tile([P, P], F32, name="res_b")
+        nc.vector.tensor_copy(out=res_b[32:64, :], in_=fb[32:64, :])
+        nc.sync.dma_start(out=out_v[0], in_=res_b[32:64, :])

@@ -20,10 +20,19 @@ P = 128
 GROUPS = 8
 TOK = 256
 GATE, KV = 0, 1
-LO, HI = 0, 1
 RNG_A, RNG_B = 0, 1
 TWO_PI_HI = 6.28125
 TWO_PI_LO = 2.0 * math.pi - TWO_PI_HI
+EW = 640
+FAR = 1.0e30
+
+
+def store_view(t):
+    return t.rearrange("p (h c) -> p h c", h=2)[:, :, 0:256].rearrange("p h (k s) -> p h k s", s=32)
+
+
+def window_view(t):
+    return t[:, 0:576].rearrange("p (h k s) -> p k h s", h=2, k=9, s=32)[:, 0:8]
 
 
 def tile_deepseekv4csacompressor_w_kernel(
@@ -35,8 +44,8 @@ def tile_deepseekv4csacompressor_w_kernel(
     with ExitStack() as ctx:
         const = ctx.enter_context(tc.tile_pool(name="const", bufs=1))
         wpool = ctx.enter_context(tc.tile_pool(name="weights", bufs=1))
-        work = ctx.enter_context(tc.tile_pool(name="work", bufs=2))
         psum = ctx.enter_context(tc.psum_pool(name="psum", bufs=1))
+        ctx.enter_context(tc.manual_schedule())
 
         ident_f = const.tile([P, P], F32, name="ident_f")
         make_identity(nc, ident_f[:])
@@ -47,12 +56,22 @@ def tile_deepseekv4csacompressor_w_kernel(
             pl = const.tile([P, 2, 2048], U8, name="planes%d" % w, align_bytes=64)
             nc.vector.memset(pl[:].bitcast(I32), 0)
             planes.append(pl)
-        pooled_t = const.tile([P, P], F32, name="pooled_t")
-        nc.gpsimd.memset(pooled_t[:], 0.0)
+        pooled = []
+        for r in range(2):
+            pt = const.tile([P, P], F32, name="pooled%d" % r)
+            nc.gpsimd.memset(pt[:], 0.0)
+            pooled.append(pt)
         freq = const.tile([P, 32], F32, name="freq")
         nc.gpsimd.memset(freq[:, 0:1], 1.0)
         row_i = const.tile([P, 1], I32, name="row_i")
         nc.gpsimd.iota(row_i[:], pattern=[[0, 1]], base=0, channel_multiplier=1)
+        e_tiles = []
+        for u in range(8):
+            e = const.tile([P, EW], F32, name="e%d" % u)
+            nc.gpsimd.memset(e[:, 288:320], FAR)
+            e_tiles.append(e)
+        prod_a = const.tile([P, 4, EW], F32, name="prod_a")
+        nc.gpsimd.memset(prod_a[:, :, 288:320], 0.0)
 
         bias_sb = const.tile([P, 512], BF16, name="bias_sb")
         nc.scalar.dma_start(out=bias_sb[:], in_=position_bias.rearrange("s (h c) -> (s h) c", h=2))
@@ -73,40 +92,36 @@ def tile_deepseekv4csacompressor_w_kernel(
                     in_=scales[w][4 * a : 4 * a + 4, 4 * q : 4 * q + 4, :].bitcast(view),
                 )
 
-        def first_col(rng, half):
-            return 1024 * half + (512 if rng == RNG_A else 0)
-
         wt = {}
 
-        def load_words(w, rng, half, group_lists):
-            c0 = first_col(rng, half)
+        def load_words(w, c0, ncols, group_lists):
             for gs in group_lists:
-                t = wpool.tile(
-                    [P, len(gs), 512], U32, name="w%d_%d_%d_%d" % (w, rng, half, gs[0]), align_bytes=64
-                )
+                t = wpool.tile([P, len(gs), ncols], U32, name="w%d_%d_%d" % (w, c0, gs[0]), align_bytes=64)
                 nc.sync.dma_start(
                     out=t[:].bitcast(I32),
-                    in_=words[w][gs[0] : gs[-1] + 1, :, c0 : c0 + 512, :]
+                    in_=words[w][gs[0] : gs[-1] + 1, :, c0 : c0 + ncols, :]
                     .rearrange("g p n t -> p g (n t)")
                     .bitcast(I32),
                 )
                 for k in range(len(gs)):
-                    wt[(w, rng, half, gs[k])] = t[:, k, :]
+                    for j in range(ncols // P):
+                        wt[(w, c0 + j * P, gs[k])] = t[:, k, j * P : (j + 1) * P]
 
         pairs = [[0, 1], [2, 3], [4, 5], [6, 7]]
         load_scales(nc.sync, I32, GATE, 0)
-        load_words(GATE, RNG_A, HI, [[0], [1], [2, 3]])
+        load_words(GATE, 1536, 512, [[0], [1], [2, 3]])
         load_scales(nc.sync, I32, GATE, 1)
-        load_words(GATE, RNG_A, HI, [[4, 5], [6, 7]])
+        load_words(GATE, 1536, 512, [[4, 5], [6, 7]])
         load_scales(nc.gpsimd, F32, KV, 0)
         load_scales(nc.gpsimd, F32, KV, 1)
-        load_words(GATE, RNG_A, LO, pairs)
-        load_words(GATE, RNG_B, HI, pairs)
-        load_words(GATE, RNG_B, LO, pairs)
-        load_words(KV, RNG_A, HI, pairs)
-        load_words(KV, RNG_A, LO, pairs)
-        load_words(KV, RNG_B, HI, pairs)
-        load_words(KV, RNG_B, LO, [[0, 1], [2, 3], [4, 5], [6], [7]])
+        load_words(GATE, 512, 512, pairs)
+        load_words(GATE, 1024, 512, pairs)
+        load_words(GATE, 0, 512, pairs)
+        load_words(KV, 1536, 512, pairs)
+        load_words(KV, 512, 512, pairs)
+        load_words(KV, 1024, 512, pairs)
+        load_words(KV, 0, 256, [[0, 1, 2, 3], [4, 5, 6, 7]])
+        load_words(KV, 256, 256, [[0, 1, 2, 3], [4, 5], [6], [7]])
 
         grouped = []
         x_codes = []
@@ -126,9 +141,9 @@ def tile_deepseekv4csacompressor_w_kernel(
             for tt in range(2):
                 src = x_sb[(tt, g // 4)][:].bitcast(F32)
                 for u in range(2):
-                    lo_w = 256 * (g % 4)
+                    w0 = 256 * (g % 4)
                     nc.tensor.transpose(
-                        xt[:, u, tt * P : (tt + 1) * P], src[:, lo_w + u : lo_w + 256 : 2], ident_f[:]
+                        xt[:, u, tt * P : (tt + 1) * P], src[:, w0 + u : w0 + 256 : 2], ident_f[:]
                     )
             dst = grouped[g][:].bitcast(F32).rearrange("p (t u) -> p t u", u=2)
             if g % 4 == 3:
@@ -204,40 +219,33 @@ def tile_deepseekv4csacompressor_w_kernel(
         nc.vector.tensor_tensor(out=red[:], in0=red[:], in1=fold[:], op=ALU.add)
         sin_cos = const.tile([P, 64], F32, name="sin_cos")
         nc.scalar.activation(out=sin_cos[:], in_=red[:], func=ACT.Sin)
+        warm = const.tile([P, 1], F32, name="warm")
+        nc.scalar.activation(out=warm[:], in_=sin_cos[:, 0:1], func=ACT.Exp)
 
-        def mx_block(w, rng, half, outs):
-            c0 = first_col(rng, half)
+        def mx_block(w, c0, outs):
             for g in range(GROUPS):
-                for j in range(4):
+                for j in range(len(outs)):
+                    c = c0 + j * P
                     nc.tensor.matmul_mx(
                         out=outs[j],
-                        lhsT=wt[(w, rng, half, g)][:, j * P : (j + 1) * P].bitcast(FP8X4),
-                        lhsT_scale=planes[w][4 * (g % 4) : P, g // 4, c0 + j * P : c0 + (j + 1) * P],
+                        lhsT=wt[(w, c, g)].bitcast(FP8X4),
+                        lhsT_scale=planes[w][4 * (g % 4) : P, g // 4, c : c + P],
                         rhs=x_codes[g][:].bitcast(FP8X4),
                         rhs_scale=x_scl[g][:],
                         start=(g == 0),
                         stop=(g == GROUPS - 1),
                     )
 
-        e_tiles = {}
-        neg_max = {}
-        sums = {}
-        rden = {}
-
-        def unit_of(rng, j):
-            return j + (4 if rng == RNG_A else 0)
+        neg_max = [const.tile([P, 4, 8], F32, name="neg_max%d" % r) for r in range(2)]
+        den = [const.tile([P, 4, 8], F32, name="den%d" % r) for r in range(2)]
+        rden = [const.tile([P, 4, 8], F32, name="rden%d" % r) for r in range(2)]
 
         def softmax_weights(rng, banks):
-            nm = const.tile([P, 4, 16], F32, name="neg_max%d" % rng)
-            sm = const.tile([P, 4, 16], F32, name="sums%d" % rng)
-            neg_max[rng] = nm
-            sums[rng] = sm
             for j in range(4):
-                u = unit_of(rng, j)
-                e = const.tile([P, 512], F32, name="e%d" % u)
-                e_tiles[u] = e
+                u = j + (4 if rng == RNG_A else 0)
+                e = e_tiles[u]
                 nc.vector.tensor_tensor(
-                    out=e[:].rearrange("p (h k s) -> p h k s", h=2, k=8),
+                    out=store_view(e[:]),
                     in0=neg_bias[:, u, :]
                     .rearrange("p (h s) -> p h s", h=2)
                     .unsqueeze(2)
@@ -246,53 +254,37 @@ def tile_deepseekv4csacompressor_w_kernel(
                     op=ALU.subtract,
                 )
                 nc.vector.tensor_reduce(
-                    out=nm[:, j, 0:15],
-                    in_=e[:, 0:480].rearrange("p (k s) -> p k s", s=32),
-                    axis=AX.X,
-                    op=ALU.min,
+                    out=neg_max[rng][:, j, :], in_=window_view(e[:]), axis=AX.XY, op=ALU.min
                 )
-                nc.vector.tensor_tensor(
-                    out=nm[:, j, 1:8], in0=nm[:, j, 1:8], in1=nm[:, j, 8:15], op=ALU.min
-                )
-                for k in range(15):
-                    win = k if k < 8 else k - 7
+                for i in range(8):
                     nc.scalar.activation(
-                        out=e[:, 32 * k : 32 * k + 32],
-                        in_=e[:, 32 * k : 32 * k + 32],
+                        out=window_view(e[:])[:, i],
+                        in_=window_view(e[:])[:, i],
                         func=ACT.Exp,
-                        bias=nm[:, j, win : win + 1],
+                        bias=neg_max[rng][:, j, i : i + 1],
                         scale=-1.0,
-                        accum_out=sm[:, j, k : k + 1],
+                        accum_out=den[rng][:, j, i : i + 1],
                     )
-            den = const.tile([P, 4, 8], F32, name="den%d" % rng)
-            nc.vector.tensor_copy(out=den[:, :, 0:1], in_=sm[:, :, 0:1])
-            nc.vector.tensor_tensor(out=den[:, :, 1:8], in0=sm[:, :, 1:8], in1=sm[:, :, 8:15], op=ALU.add)
-            rd = const.tile([P, 4, 8], F32, name="rden%d" % rng)
-            nc.vector.reciprocal(out=rd[:], in_=den[:])
-            rden[rng] = rd
-
-        def finish(rng, num):
-            nc.vector.tensor_tensor(out=num[:, :, 1:8], in0=num[:, :, 1:8], in1=num[:, :, 8:15], op=ALU.add)
-            nc.vector.tensor_tensor(
-                out=pooled_t[:, 32 * rng : 32 * rng + 32].rearrange("p (i j) -> p j i", j=4),
-                in0=num[:, :, 0:8],
-                in1=rden[rng][:],
-                op=ALU.mult,
-            )
 
         out_v = out[0].rearrange("i (h j c) -> h i j c", h=2, j=4)
 
-        for rng in (RNG_A, RNG_B):
-            banks = [
-                psum.tile([P, 512], F32, tag="bank%d" % (4 * rng + j), name="gate%d_%d" % (rng, j))
-                for j in range(4)
-            ]
-            mx_block(GATE, rng, HI, [b[:, 0:256] for b in banks])
-            mx_block(GATE, rng, LO, [b[:, 256:512] for b in banks])
-            softmax_weights(rng, banks)
+        gate_a = [psum.tile([P, 512], F32, tag="bank%d" % j, name="gate_a%d" % j) for j in range(4)]
+        mx_block(GATE, 1536, [b[:, 0:256] for b in gate_a])
+        mx_block(GATE, 512, [b[:, 256:512] for b in gate_a])
+        gate_b = [psum.tile([P, 512], F32, tag="bank%d" % (4 + j), name="gate_b%d" % j) for j in range(4)]
+        mx_block(GATE, 1024, [b[:, 0:256] for b in gate_b])
+        mx_block(GATE, 0, [b[:, 256:512] for b in gate_b])
+        softmax_weights(RNG_A, gate_a)
+        nc.vector.reciprocal(out=rden[RNG_A][:], in_=den[RNG_A][:])
 
+        kv_a = [psum.tile([P, 512], F32, tag="bank%d" % j, name="kv_a%d" % j) for j in range(4)]
+        mx_block(KV, 1536, [b[:, 0:256] for b in kv_a])
+        mx_block(KV, 512, [b[:, 256:512] for b in kv_a])
+
+        softmax_weights(RNG_B, gate_b)
+        nc.vector.reciprocal(out=rden[RNG_B][:], in_=den[RNG_B][:])
         for j in range(4):
-            e_lo = e_tiles[j][:, 256:480].rearrange("p (k s) -> p k s", s=32)
+            e_lo = e_tiles[j][:, 320:544].rearrange("p (k s) -> p k s", s=32)
             nc.vector.tensor_tensor(
                 out=e_lo,
                 in0=e_lo,
@@ -300,39 +292,39 @@ def tile_deepseekv4csacompressor_w_kernel(
                 op=ALU.mult,
             )
 
-        banks = [psum.tile([P, 512], F32, tag="bank%d" % j, name="kv_a%d" % j) for j in range(4)]
-        mx_block(KV, RNG_A, HI, [b[:, 0:256] for b in banks])
-        mx_block(KV, RNG_A, LO, [b[:, 256:512] for b in banks])
-        prod = work.tile([P, 4, 512], F32, tag="prod", name="prod_a")
-        for j in range(4):
-            nc.vector.tensor_tensor(
-                out=prod[:, j, 0:480], in0=banks[j][:, 0:480], in1=e_tiles[4 + j][:, 0:480], op=ALU.mult
-            )
-        num_a = const.tile([P, 4, 16], F32, name="num_a")
-        nc.vector.tensor_reduce(
-            out=num_a[:, :, 0:15],
-            in_=prod[:, :, 0:480].rearrange("p j (k s) -> p j k s", s=32),
-            axis=AX.X,
-            op=ALU.add,
-        )
-        finish(RNG_A, num_a)
+        kv_bh = [psum.tile([P, 256], F32, tag="bank%d" % (4 + j), name="kv_bh%d" % j) for j in range(4)]
+        mx_block(KV, 1024, [b[:] for b in kv_bh])
 
-        num_b = const.tile([P, 4, 16], F32, name="num_b")
-        banks = [psum.tile([P, 256], F32, tag="bank%d" % (4 + j), name="kv_bh%d" % j) for j in range(4)]
-        mx_block(KV, RNG_B, HI, [b[:] for b in banks])
-        prod = work.tile([P, 4, 512], F32, tag="prod", name="prod_bh")
         for j in range(4):
             nc.vector.tensor_tensor(
-                out=prod[:, j, 0:256], in0=banks[j][:], in1=e_tiles[j][:, 0:256], op=ALU.mult
+                out=store_view(prod_a[:, j, :]),
+                in0=kv_a[j][:].rearrange("p (h k s) -> p h k s", h=2, k=8),
+                in1=store_view(e_tiles[4 + j][:]),
+                op=ALU.mult,
+            )
+        num_a = const.tile([P, 4, 8], F32, name="num_a")
+        for j in range(4):
+            nc.vector.tensor_reduce(
+                out=num_a[:, j, :], in_=window_view(prod_a[:, j, :]), axis=AX.XY, op=ALU.add
+            )
+        nc.vector.tensor_tensor(
+            out=pooled[RNG_A][:, 0:32].rearrange("p (i j) -> p j i", j=4),
+            in0=num_a[:],
+            in1=rden[RNG_A][:],
+            op=ALU.mult,
+        )
+
+        num_b = const.tile([P, 4, 8], F32, name="num_b")
+        prod_bh = const.tile([P, 4, 256], F32, name="prod_bh")
+        for j in range(4):
+            nc.vector.tensor_tensor(
+                out=prod_bh[:, j, :], in0=kv_bh[j][:], in1=e_tiles[j][:, 0:256], op=ALU.mult
             )
         nc.vector.tensor_reduce(
-            out=num_b[:, :, 0:8],
-            in_=prod[:, :, 0:256].rearrange("p j (k s) -> p j k s", s=32),
-            axis=AX.X,
-            op=ALU.add,
+            out=num_b[:], in_=prod_bh[:].rearrange("p j (k s) -> p j k s", s=32), axis=AX.X, op=ALU.add
         )
         prod_bl = const.tile([P, 4, 7, 33], F32, name="prod_bl")
-        pooled_b = pooled_t[:, 32:64].rearrange("p (i j) -> p j i", j=4)
+        pooled_b = pooled[RNG_B][:, 0:32].rearrange("p (i j) -> p j i", j=4)
         nc.vector.tensor_tensor(
             out=prod_bl[:, :, :, 32], in0=num_b[:, :, 1:8], in1=rden[RNG_B][:, :, 1:8], op=ALU.mult
         )
@@ -340,36 +332,43 @@ def tile_deepseekv4csacompressor_w_kernel(
             out=pooled_b[:, :, 0], in0=num_b[:, :, 0], in1=rden[RNG_B][:, :, 0], op=ALU.mult
         )
 
+        kv_bl = [psum.tile([P, 256], F32, tag="bank%d" % j, name="kv_bl%d" % j) for j in range(4)]
+        mx_block(KV, 0, [b[:] for b in kv_bl[0:2]])
         fa = psum.tile([P, P], F32, tag="bank4", name="fa")
-        nc.tensor.transpose(fa[:], pooled_t[:], ident_f[:])
+        nc.tensor.transpose(fa[:], pooled[RNG_A][:], ident_f[:])
+        mx_block(KV, 256, [b[:] for b in kv_bl[2:4]])
+
+        R = 32
         res_a = const.tile([P, P], F32, name="res_a")
         t_cos = const.tile([P, 32, 2], F32, name="t_cos")
         t_sin = const.tile([P, 32, 2], F32, name="t_sin")
-        R = 32
-        v = fa[0:R, 64:128].rearrange("p (j e) -> p j e", e=2)
-        o = res_a[0:R, 64:128].rearrange("p (j e) -> p j e", e=2)
-        nc.vector.tensor_copy(out=res_a[0:R, 0:64], in_=fa[0:R, 0:64])
-        nc.vector.tensor_tensor(
+        nc.scalar.copy(out=res_a[0:R, :], in_=fa[0:R, :])
+        v = res_a[0:R, 64:128].rearrange("p (j e) -> p j e", e=2)
+        nc.gpsimd.tensor_tensor(
             out=t_cos[0:R], in0=v, in1=sin_cos[0:R, 32:64].unsqueeze(2).to_broadcast([R, 32, 2]), op=ALU.mult
         )
-        nc.vector.tensor_tensor(out=t_sin[0:R, :, 0], in0=v[:, :, 1], in1=sin_cos[0:R, 0:32], op=ALU.mult)
-        nc.vector.tensor_tensor(out=t_sin[0:R, :, 1], in0=v[:, :, 0], in1=sin_cos[0:R, 0:32], op=ALU.mult)
-        nc.vector.tensor_tensor(out=o[:, :, 0], in0=t_cos[0:R, :, 0], in1=t_sin[0:R, :, 0], op=ALU.subtract)
-        nc.vector.tensor_tensor(out=o[:, :, 1], in0=t_cos[0:R, :, 1], in1=t_sin[0:R, :, 1], op=ALU.add)
+        nc.gpsimd.tensor_tensor(out=t_sin[0:R, :, 0], in0=v[:, :, 1], in1=sin_cos[0:R, 0:32], op=ALU.mult)
+        nc.gpsimd.tensor_tensor(out=t_sin[0:R, :, 1], in0=v[:, :, 0], in1=sin_cos[0:R, 0:32], op=ALU.mult)
+        nc.gpsimd.tensor_tensor(out=v[:, :, 0], in0=t_cos[0:R, :, 0], in1=t_sin[0:R, :, 0], op=ALU.subtract)
+        nc.gpsimd.tensor_tensor(out=v[:, :, 1], in0=t_cos[0:R, :, 1], in1=t_sin[0:R, :, 1], op=ALU.add)
         nc.gpsimd.dma_start(out=out_v[1], in_=res_a[0:R, :])
 
-        banks = [psum.tile([P, 256], F32, tag="bank%d" % j, name="kv_bl%d" % j) for j in range(4)]
-        mx_block(KV, RNG_B, LO, [b[:] for b in banks])
-        for j in range(4):
-            nc.vector.tensor_tensor(
-                out=prod_bl[:, j, :, 0:32],
-                in0=banks[j][:, 0:224].rearrange("p (k s) -> p k s", s=32),
-                in1=e_tiles[j][:, 256:480].rearrange("p (k s) -> p k s", s=32),
-                op=ALU.mult,
+        for pair in range(2):
+            for j in (2 * pair, 2 * pair + 1):
+                nc.vector.tensor_tensor(
+                    out=prod_bl[:, j, :, 0:32],
+                    in0=kv_bl[j][:, 0:224].rearrange("p (k s) -> p k s", s=32),
+                    in1=e_tiles[j][:, 320:544].rearrange("p (k s) -> p k s", s=32),
+                    op=ALU.mult,
+                )
+            nc.vector.tensor_reduce(
+                out=pooled_b[:, 2 * pair : 2 * pair + 2, 1:8],
+                in_=prod_bl[:, 2 * pair : 2 * pair + 2],
+                axis=AX.X,
+                op=ALU.add,
             )
-        nc.vector.tensor_reduce(out=pooled_b[:, :, 1:8], in_=prod_bl[:], axis=AX.X, op=ALU.add)
         fb = psum.tile([P, P], F32, tag="bank5", name="fb")
-        nc.tensor.transpose(fb[:], pooled_t[:], ident_f[:])
+        nc.tensor.transpose(fb[:], pooled[RNG_B][:], ident_f[:])
         res_b = const.tile([P, P], F32, name="res_b")
-        nc.vector.tensor_copy(out=res_b[32:64, :], in_=fb[32:64, :])
-        nc.sync.dma_start(out=out_v[0], in_=res_b[32:64, :])
+        nc.vector.tensor_copy(out=res_b[0:R, :], in_=fb[0:R, :])
+        nc.sync.dma_start(out=out_v[0], in_=res_b[0:R, :])

@@ -86,7 +86,7 @@ def tile_deepseekv4csacompressor_w_kernel(
                 x_sb[(tt, half)] = xs
 
         def load_scales(queue, view, w, a):
-            for q in range(4):
+            for q in (0, 2, 1, 3):
                 queue.dma_start(
                     out=planes[w][32 * q : 32 * q + 16, a, :].bitcast(view),
                     in_=scales[w][4 * a : 4 * a + 4, 4 * q : 4 * q + 4, :].bitcast(view),
@@ -109,19 +109,30 @@ def tile_deepseekv4csacompressor_w_kernel(
 
         pairs = [[0, 1], [2, 3], [4, 5], [6, 7]]
         load_scales(nc.sync, I32, GATE, 0)
-        load_words(GATE, 1536, 512, [[0], [1], [2, 3]])
+        load_words(GATE, 0, 2048, [[0], [1]])
         load_scales(nc.sync, I32, GATE, 1)
-        load_words(GATE, 1536, 512, [[4, 5], [6, 7]])
-        load_scales(nc.gpsimd, F32, KV, 0)
-        load_scales(nc.gpsimd, F32, KV, 1)
-        load_words(GATE, 512, 512, pairs)
-        load_words(GATE, 1024, 512, pairs)
-        load_words(GATE, 0, 512, pairs)
-        load_words(KV, 1536, 512, pairs)
+        load_words(GATE, 0, 2048, [[g] for g in range(2, GROUPS)])
+        load_scales(nc.sync, I32, KV, 0)
+        load_words(KV, 1536, 512, [[0, 1]])
+        load_scales(nc.sync, I32, KV, 1)
+        load_words(KV, 1536, 512, [[2, 3], [4, 5], [6, 7]])
         load_words(KV, 512, 512, pairs)
         load_words(KV, 1024, 512, pairs)
-        load_words(KV, 0, 256, [[0, 1, 2, 3], [4, 5, 6, 7]])
-        load_words(KV, 256, 256, [[0, 1, 2, 3], [4, 5], [6], [7]])
+        load_words(KV, 0, 256, pairs)
+        load_words(KV, 256, 256, [[0, 1], [2, 3], [4, 5], [6], [7]])
+
+        bt = psum.tile([P, 4, P], BF16, tag="bank7", name="bt")
+        for b in range(4):
+            nc.tensor.transpose(bt[:, b, :], bias_sb[:, b * P : (b + 1) * P], ident_b[:])
+        neg_bias = const.tile([P, 8, 64], F32, name="neg_bias")
+        bt_v = bt[:].rearrange("p b (s h) -> p h b s", h=2)
+        nb_v = neg_bias[:].rearrange("p (h b) s -> p h b s", h=2)
+        nc.vector.tensor_scalar(
+            out=nb_v[:, :, :, 0:32], in0=bt_v[:, :, :, 32:64], scalar1=-1.0, scalar2=None, op0=ALU.mult
+        )
+        nc.vector.tensor_scalar(
+            out=nb_v[:, :, :, 32:64], in0=bt_v[:, :, :, 0:32], scalar1=-1.0, scalar2=None, op0=ALU.mult
+        )
 
         grouped = []
         x_codes = []
@@ -153,19 +164,6 @@ def tile_deepseekv4csacompressor_w_kernel(
             if g >= 1:
                 quantise(g - 1)
         quantise(GROUPS - 1)
-
-        bt = psum.tile([P, 4, P], BF16, tag="bank7", name="bt")
-        for b in range(4):
-            nc.tensor.transpose(bt[:, b, :], bias_sb[:, b * P : (b + 1) * P], ident_b[:])
-        neg_bias = const.tile([P, 8, 64], F32, name="neg_bias")
-        bt_v = bt[:].rearrange("p b (s h) -> p h b s", h=2)
-        nb_v = neg_bias[:].rearrange("p (h b) s -> p h b s", h=2)
-        nc.vector.tensor_scalar(
-            out=nb_v[:, :, :, 0:32], in0=bt_v[:, :, :, 32:64], scalar1=-1.0, scalar2=None, op0=ALU.mult
-        )
-        nc.vector.tensor_scalar(
-            out=nb_v[:, :, :, 32:64], in0=bt_v[:, :, :, 0:32], scalar1=-1.0, scalar2=None, op0=ALU.mult
-        )
 
         win_i = const.tile([P, 1], I32, name="win_i")
         nc.vector.tensor_scalar(
@@ -240,57 +238,57 @@ def tile_deepseekv4csacompressor_w_kernel(
         den = [const.tile([P, 4, 8], F32, name="den%d" % r) for r in range(2)]
         rden = [const.tile([P, 4, 8], F32, name="rden%d" % r) for r in range(2)]
 
-        def softmax_weights(rng, banks):
-            for j in range(4):
-                u = j + (4 if rng == RNG_A else 0)
-                e = e_tiles[u]
-                nc.vector.tensor_tensor(
-                    out=store_view(e[:]),
-                    in0=neg_bias[:, u, :]
-                    .rearrange("p (h s) -> p h s", h=2)
-                    .unsqueeze(2)
-                    .to_broadcast([P, 2, 8, 32]),
-                    in1=banks[j][:].rearrange("p (h k s) -> p h k s", h=2, k=8),
-                    op=ALU.subtract,
+        def minus_logits(u, bank):
+            nc.vector.tensor_tensor(
+                out=store_view(e_tiles[u][:]),
+                in0=neg_bias[:, u, :].rearrange("p (h s) -> p h s", h=2).unsqueeze(2).to_broadcast([P, 2, 8, 32]),
+                in1=bank[:].rearrange("p (h k s) -> p h k s", h=2, k=8),
+                op=ALU.subtract,
+            )
+
+        def weights(u):
+            rng, j = (RNG_A, u - 4) if u >= 4 else (RNG_B, u)
+            win = window_view(e_tiles[u][:])
+            nc.vector.tensor_reduce(out=neg_max[rng][:, j, :], in_=win, axis=AX.XY, op=ALU.min)
+            for i in range(8):
+                nc.scalar.activation(
+                    out=win[:, i],
+                    in_=win[:, i],
+                    func=ACT.Exp,
+                    bias=neg_max[rng][:, j, i : i + 1],
+                    scale=-1.0,
+                    accum_out=den[rng][:, j, i : i + 1],
                 )
-                nc.vector.tensor_reduce(
-                    out=neg_max[rng][:, j, :], in_=window_view(e[:]), axis=AX.XY, op=ALU.min
-                )
-                for i in range(8):
-                    nc.scalar.activation(
-                        out=window_view(e[:])[:, i],
-                        in_=window_view(e[:])[:, i],
-                        func=ACT.Exp,
-                        bias=neg_max[rng][:, j, i : i + 1],
-                        scale=-1.0,
-                        accum_out=den[rng][:, j, i : i + 1],
-                    )
 
         out_v = out[0].rearrange("i (h j c) -> h i j c", h=2, j=4)
 
-        gate_a = [psum.tile([P, 512], F32, tag="bank%d" % j, name="gate_a%d" % j) for j in range(4)]
-        mx_block(GATE, 1536, [b[:, 0:256] for b in gate_a])
-        mx_block(GATE, 512, [b[:, 256:512] for b in gate_a])
-        gate_b = [psum.tile([P, 512], F32, tag="bank%d" % (4 + j), name="gate_b%d" % j) for j in range(4)]
-        mx_block(GATE, 1024, [b[:, 0:256] for b in gate_b])
-        mx_block(GATE, 0, [b[:, 256:512] for b in gate_b])
-        softmax_weights(RNG_A, gate_a)
-        nc.vector.reciprocal(out=rden[RNG_A][:], in_=den[RNG_A][:])
+        gate = [psum.tile([P, 512], F32, tag="bank%d" % b, name="gate%d" % b) for b in range(8)]
+        for g in range(GROUPS):
+            for b in range(8):
+                for half in (1, 0):
+                    c = 1024 * half + P * ((b + 4) % 8)
+                    nc.tensor.matmul_mx(
+                        out=gate[b][:, 0:256] if half == 1 else gate[b][:, 256:512],
+                        lhsT=wt[(GATE, c, g)].bitcast(FP8X4),
+                        lhsT_scale=planes[GATE][4 * (g % 4) : P, g // 4, c : c + P],
+                        rhs=x_codes[g][:].bitcast(FP8X4),
+                        rhs_scale=x_scl[g][:],
+                        start=(g == 0 and half == 1),
+                        stop=(g == GROUPS - 1 and half == 0),
+                    )
+        for u in (4, 5, 6, 7):
+            minus_logits(u, gate[u - 4])
+        for u in (4, 5, 6, 7):
+            weights(u)
 
         kv_a = [psum.tile([P, 512], F32, tag="bank%d" % j, name="kv_a%d" % j) for j in range(4)]
         mx_block(KV, 1536, [b[:, 0:256] for b in kv_a])
         mx_block(KV, 512, [b[:, 256:512] for b in kv_a])
 
-        softmax_weights(RNG_B, gate_b)
-        nc.vector.reciprocal(out=rden[RNG_B][:], in_=den[RNG_B][:])
-        for j in range(4):
-            e_lo = e_tiles[j][:, 320:544].rearrange("p (k s) -> p k s", s=32)
-            nc.vector.tensor_tensor(
-                out=e_lo,
-                in0=e_lo,
-                in1=rden[RNG_B][:, j, 1:8].unsqueeze(2).to_broadcast([P, 7, 32]),
-                op=ALU.mult,
-            )
+        for u in (0, 1, 2, 3):
+            minus_logits(u, gate[u + 4])
+            weights(u)
+        nc.vector.reciprocal(out=rden[RNG_A][:], in_=den[RNG_A][:])
 
         kv_bh = [psum.tile([P, 256], F32, tag="bank%d" % (4 + j), name="kv_bh%d" % j) for j in range(4)]
         mx_block(KV, 1024, [b[:] for b in kv_bh])
@@ -306,6 +304,16 @@ def tile_deepseekv4csacompressor_w_kernel(
         for j in range(4):
             nc.vector.tensor_reduce(
                 out=num_a[:, j, :], in_=window_view(prod_a[:, j, :]), axis=AX.XY, op=ALU.add
+            )
+            if j == 0:
+                nc.vector.reciprocal(out=rden[RNG_B][:], in_=den[RNG_B][:])
+        for j in range(4):
+            e_lo = e_tiles[j][:, 320:544].rearrange("p (k s) -> p k s", s=32)
+            nc.gpsimd.tensor_tensor(
+                out=e_lo,
+                in0=e_lo,
+                in1=rden[RNG_B][:, j, 1:8].unsqueeze(2).to_broadcast([P, 7, 32]),
+                op=ALU.mult,
             )
         nc.vector.tensor_tensor(
             out=pooled[RNG_A][:, 0:32].rearrange("p (i j) -> p j i", j=4),

@@ -56,22 +56,10 @@ def tile_deepseekv4csacompressor_w_kernel(
             pl = const.tile([P, 2, 2048], U8, name="planes%d" % w, align_bytes=64)
             nc.vector.memset(pl[:].bitcast(I32), 0)
             planes.append(pl)
-        pooled = []
-        for r in range(2):
-            pt = const.tile([P, P], F32, name="pooled%d" % r)
-            nc.gpsimd.memset(pt[:], 0.0)
-            pooled.append(pt)
         freq = const.tile([P, 32], F32, name="freq")
         nc.gpsimd.memset(freq[:, 0:1], 1.0)
         row_i = const.tile([P, 1], I32, name="row_i")
         nc.gpsimd.iota(row_i[:], pattern=[[0, 1]], base=0, channel_multiplier=1)
-        e_tiles = []
-        for u in range(8):
-            e = const.tile([P, EW], F32, name="e%d" % u)
-            nc.gpsimd.memset(e[:, 288:320], FAR)
-            e_tiles.append(e)
-        prod_a = const.tile([P, 4, EW], F32, name="prod_a")
-        nc.gpsimd.memset(prod_a[:, :, 288:320], 0.0)
 
         bias_sb = const.tile([P, 512], BF16, name="bias_sb")
         nc.scalar.dma_start(out=bias_sb[:], in_=position_bias.rearrange("s (h c) -> (s h) c", h=2))
@@ -108,18 +96,28 @@ def tile_deepseekv4csacompressor_w_kernel(
                         wt[(w, c0 + j * P, gs[k])] = t[:, k, j * P : (j + 1) * P]
 
         pairs = [[0, 1], [2, 3], [4, 5], [6, 7]]
-        load_scales(nc.sync, I32, GATE, 0)
-        load_words(GATE, 0, 2048, [[0], [1]])
-        load_scales(nc.sync, I32, GATE, 1)
-        load_words(GATE, 0, 2048, [[g] for g in range(2, GROUPS)])
-        load_scales(nc.sync, I32, KV, 0)
-        load_words(KV, 1536, 512, [[0, 1]])
-        load_scales(nc.sync, I32, KV, 1)
-        load_words(KV, 1536, 512, [[2, 3], [4, 5], [6, 7]])
+        for w in (GATE, KV):
+            for a in range(2):
+                load_scales(nc.gpsimd, F32, w, a)
+        load_words(GATE, 0, 2048, [[g] for g in range(GROUPS)])
+        load_words(KV, 1536, 512, pairs)
         load_words(KV, 512, 512, pairs)
         load_words(KV, 1024, 512, pairs)
         load_words(KV, 0, 256, pairs)
         load_words(KV, 256, 256, [[0, 1], [2, 3], [4, 5], [6], [7]])
+
+        pooled = []
+        for r in range(2):
+            pt = const.tile([P, P], F32, name="pooled%d" % r)
+            nc.gpsimd.memset(pt[:], 0.0)
+            pooled.append(pt)
+        e_tiles = []
+        for u in range(8):
+            e = const.tile([P, EW], F32, name="e%d" % u)
+            nc.gpsimd.memset(e[:, 288:320], FAR)
+            e_tiles.append(e)
+        prod_a = const.tile([P, 4, EW], F32, name="prod_a")
+        nc.gpsimd.memset(prod_a[:, :, 288:320], 0.0)
 
         bt = psum.tile([P, 4, P], BF16, tag="bank7", name="bt")
         for b in range(4):

@@ -96,9 +96,10 @@ def tile_deepseekv4csacompressor_w_kernel(
                         wt[(w, c0 + j * P, gs[k])] = t[:, k, j * P : (j + 1) * P]
 
         pairs = [[0, 1], [2, 3], [4, 5], [6, 7]]
-        for w in (GATE, KV):
-            for a in range(2):
-                load_scales(nc.gpsimd, F32, w, a)
+        load_scales(nc.sync, I32, GATE, 0)
+        load_scales(nc.gpsimd, F32, GATE, 1)
+        load_scales(nc.gpsimd, F32, KV, 0)
+        load_scales(nc.gpsimd, F32, KV, 1)
         load_words(GATE, 0, 2048, [[g] for g in range(GROUPS)])
         load_words(KV, 1536, 512, pairs)
         load_words(KV, 512, 512, pairs)

@@ -56,15 +56,28 @@ def tile_deepseekv4csacompressor_w_kernel(
             pl = const.tile([P, 2, 2048], U8, name="planes%d" % w, align_bytes=64)
             nc.vector.memset(pl[:].bitcast(I32), 0)
             planes.append(pl)
+        pooled = []
+        for r in range(2):
+            pt = const.tile([P, P], F32, name="pooled%d" % r)
+            nc.gpsimd.memset(pt[:], 0.0)
+            pooled.append(pt)
         freq = const.tile([P, 32], F32, name="freq")
         nc.gpsimd.memset(freq[:, 0:1], 1.0)
         row_i = const.tile([P, 1], I32, name="row_i")
         nc.gpsimd.iota(row_i[:], pattern=[[0, 1]], base=0, channel_multiplier=1)
+        e_tiles = []
+        for u in range(8):
+            e = const.tile([P, EW], F32, name="e%d" % u)
+            nc.gpsimd.memset(e[:, 288:320], FAR)
+            e_tiles.append(e)
+        prod_a = const.tile([P, 4, EW], F32, name="prod_a")
+        nc.gpsimd.memset(prod_a[:, :, 288:320], 0.0)
 
         bias_sb = const.tile([P, 512], BF16, name="bias_sb")
         nc.scalar.dma_start(out=bias_sb[:], in_=position_bias.rearrange("s (h c) -> (s h) c", h=2))
         x_sb = {}
-        for half in range(2):
+
+        def load_x(half):
             for tt in range(2):
                 xs = const.tile([P, 2048], BF16, name="x_sb%d_%d" % (tt, half))
                 nc.sync.dma_start(
@@ -74,7 +87,7 @@ def tile_deepseekv4csacompressor_w_kernel(
                 x_sb[(tt, half)] = xs
 
         def load_scales(queue, view, w, a):
-            for q in (0, 2, 1, 3):
+            for q in range(4):
                 queue.dma_start(
                     out=planes[w][32 * q : 32 * q + 16, a, :].bitcast(view),
                     in_=scales[w][4 * a : 4 * a + 4, 4 * q : 4 * q + 4, :].bitcast(view),
@@ -96,29 +109,23 @@ def tile_deepseekv4csacompressor_w_kernel(
                         wt[(w, c0 + j * P, gs[k])] = t[:, k, j * P : (j + 1) * P]
 
         pairs = [[0, 1], [2, 3], [4, 5], [6, 7]]
+        load_x(0)
         load_scales(nc.sync, I32, GATE, 0)
-        load_scales(nc.gpsimd, F32, GATE, 1)
+        load_words(GATE, 1536, 512, [[0], [1]])
+        load_x(1)
+        load_words(GATE, 1536, 512, [[2, 3]])
+        load_scales(nc.sync, I32, GATE, 1)
+        load_words(GATE, 1536, 512, [[4, 5], [6, 7]])
         load_scales(nc.gpsimd, F32, KV, 0)
         load_scales(nc.gpsimd, F32, KV, 1)
-        load_words(GATE, 0, 2048, [[g] for g in range(GROUPS)])
+        load_words(GATE, 512, 512, pairs)
+        load_words(GATE, 1024, 512, pairs)
+        load_words(GATE, 0, 512, pairs)
         load_words(KV, 1536, 512, pairs)
         load_words(KV, 512, 512, pairs)
         load_words(KV, 1024, 512, pairs)
-        load_words(KV, 0, 256, pairs)
-        load_words(KV, 256, 256, [[0, 1], [2, 3], [4, 5], [6], [7]])
-
-        pooled = []
-        for r in range(2):
-            pt = const.tile([P, P], F32, name="pooled%d" % r)
-            nc.gpsimd.memset(pt[:], 0.0)
-            pooled.append(pt)
-        e_tiles = []
-        for u in range(8):
-            e = const.tile([P, EW], F32, name="e%d" % u)
-            nc.gpsimd.memset(e[:, 288:320], FAR)
-            e_tiles.append(e)
-        prod_a = const.tile([P, 4, EW], F32, name="prod_a")
-        nc.gpsimd.memset(prod_a[:, :, 288:320], 0.0)
+        load_words(KV, 0, 256, [[0, 1, 2, 3], [4, 5, 6, 7]])
+        load_words(KV, 256, 256, [[0, 1, 2, 3], [4, 5], [6], [7]])
 
         bt = psum.tile([P, 4, P], BF16, tag="bank7", name="bt")
         for b in range(4):
@@ -146,23 +153,44 @@ def tile_deepseekv4csacompressor_w_kernel(
                 out=x_codes[g][:].bitcast(FP8X4), scales=x_scl[g][:], in_=grouped[g][:]
             )
 
-        for g in range(GROUPS):
-            xt = psum.tile([P, 2, TOK], F32, tag="bank%d" % g, name="xt%d" % g)
-            for tt in range(2):
-                src = x_sb[(tt, g // 4)][:].bitcast(F32)
-                for u in range(2):
-                    w0 = 256 * (g % 4)
-                    nc.tensor.transpose(
-                        xt[:, u, tt * P : (tt + 1) * P], src[:, w0 + u : w0 + 256 : 2], ident_f[:]
+        def prepare_x(half):
+            for g in range(4 * half, 4 * half + 4):
+                xt = psum.tile([P, 2, TOK], F32, tag="bank%d" % (4 + g % 4), name="xt%d" % g)
+                for tt in range(2):
+                    src = x_sb[(tt, half)][:].bitcast(F32)
+                    for u in range(2):
+                        w0 = 256 * (g % 4)
+                        nc.tensor.transpose(
+                            xt[:, u, tt * P : (tt + 1) * P], src[:, w0 + u : w0 + 256 : 2], ident_f[:]
+                        )
+                dst = grouped[g][:].bitcast(F32).rearrange("p (t u) -> p t u", u=2)
+                if g % 4 == 3:
+                    nc.vector.tensor_copy(out=dst, in_=xt[:].rearrange("p u t -> p t u"))
+                else:
+                    nc.scalar.copy(out=dst, in_=xt[:].rearrange("p u t -> p t u"))
+                if g % 4 >= 1:
+                    quantise(g - 1)
+            quantise(4 * half + 3)
+
+        def mx_block(w, c0, outs, groups):
+            for g in groups:
+                for j in range(len(outs)):
+                    c = c0 + j * P
+                    nc.tensor.matmul_mx(
+                        out=outs[j],
+                        lhsT=wt[(w, c, g)].bitcast(FP8X4),
+                        lhsT_scale=planes[w][4 * (g % 4) : P, g // 4, c : c + P],
+                        rhs=x_codes[g][:].bitcast(FP8X4),
+                        rhs_scale=x_scl[g][:],
+                        start=(g == 0),
+                        stop=(g == GROUPS - 1),
                     )
-            dst = grouped[g][:].bitcast(F32).rearrange("p (t u) -> p t u", u=2)
-            if g % 4 == 3:
-                nc.vector.tensor_copy(out=dst, in_=xt[:].rearrange("p u t -> p t u"))
-            else:
-                nc.scalar.copy(out=dst, in_=xt[:].rearrange("p u t -> p t u"))
-            if g >= 1:
-                quantise(g - 1)
-        quantise(GROUPS - 1)
+
+        every = list(range(GROUPS))
+        prepare_x(0)
+        gate_a = [psum.tile([P, 512], F32, tag="bank%d" % j, name="gate_a%d" % j) for j in range(4)]
+        mx_block(GATE, 1536, [b[:, 0:256] for b in gate_a], [0, 1])
+        prepare_x(1)
 
         win_i = const.tile([P, 1], I32, name="win_i")
         nc.vector.tensor_scalar(
@@ -219,78 +247,63 @@ def tile_deepseekv4csacompressor_w_kernel(
         warm = const.tile([P, 1], F32, name="warm")
         nc.scalar.activation(out=warm[:], in_=sin_cos[:, 0:1], func=ACT.Exp)
 
-        def mx_block(w, c0, outs):
-            for g in range(GROUPS):
-                for j in range(len(outs)):
-                    c = c0 + j * P
-                    nc.tensor.matmul_mx(
-                        out=outs[j],
-                        lhsT=wt[(w, c, g)].bitcast(FP8X4),
-                        lhsT_scale=planes[w][4 * (g % 4) : P, g // 4, c : c + P],
-                        rhs=x_codes[g][:].bitcast(FP8X4),
-                        rhs_scale=x_scl[g][:],
-                        start=(g == 0),
-                        stop=(g == GROUPS - 1),
-                    )
-
         neg_max = [const.tile([P, 4, 8], F32, name="neg_max%d" % r) for r in range(2)]
         den = [const.tile([P, 4, 8], F32, name="den%d" % r) for r in range(2)]
         rden = [const.tile([P, 4, 8], F32, name="rden%d" % r) for r in range(2)]
 
-        def minus_logits(u, bank):
-            nc.vector.tensor_tensor(
-                out=store_view(e_tiles[u][:]),
-                in0=neg_bias[:, u, :].rearrange("p (h s) -> p h s", h=2).unsqueeze(2).to_broadcast([P, 2, 8, 32]),
-                in1=bank[:].rearrange("p (h k s) -> p h k s", h=2, k=8),
-                op=ALU.subtract,
-            )
-
-        def weights(u):
-            rng, j = (RNG_A, u - 4) if u >= 4 else (RNG_B, u)
-            win = window_view(e_tiles[u][:])
-            nc.vector.tensor_reduce(out=neg_max[rng][:, j, :], in_=win, axis=AX.XY, op=ALU.min)
-            for i in range(8):
-                nc.scalar.activation(
-                    out=win[:, i],
-                    in_=win[:, i],
-                    func=ACT.Exp,
-                    bias=neg_max[rng][:, j, i : i + 1],
-                    scale=-1.0,
-                    accum_out=den[rng][:, j, i : i + 1],
+        def softmax_weights(rng, banks):
+            for j in range(4):
+                u = j + (4 if rng == RNG_A else 0)
+                e = e_tiles[u]
+                nc.vector.tensor_tensor(
+                    out=store_view(e[:]),
+                    in0=neg_bias[:, u, :]
+                    .rearrange("p (h s) -> p h s", h=2)
+                    .unsqueeze(2)
+                    .to_broadcast([P, 2, 8, 32]),
+                    in1=banks[j][:].rearrange("p (h k s) -> p h k s", h=2, k=8),
+                    op=ALU.subtract,
                 )
+                nc.vector.tensor_reduce(
+                    out=neg_max[rng][:, j, :], in_=window_view(e[:]), axis=AX.XY, op=ALU.min
+                )
+                for i in range(8):
+                    nc.scalar.activation(
+                        out=window_view(e[:])[:, i],
+                        in_=window_view(e[:])[:, i],
+                        func=ACT.Exp,
+                        bias=neg_max[rng][:, j, i : i + 1],
+                        scale=-1.0,
+                        accum_out=den[rng][:, j, i : i + 1],
+                    )
 
         out_v = out[0].rearrange("i (h j c) -> h i j c", h=2, j=4)
 
-        gate = [psum.tile([P, 512], F32, tag="bank%d" % b, name="gate%d" % b) for b in range(8)]
-        for g in range(GROUPS):
-            for b in range(8):
-                for half in (1, 0):
-                    c = 1024 * half + P * ((b + 4) % 8)
-                    nc.tensor.matmul_mx(
-                        out=gate[b][:, 0:256] if half == 1 else gate[b][:, 256:512],
-                        lhsT=wt[(GATE, c, g)].bitcast(FP8X4),
-                        lhsT_scale=planes[GATE][4 * (g % 4) : P, g // 4, c : c + P],
-                        rhs=x_codes[g][:].bitcast(FP8X4),
-                        rhs_scale=x_scl[g][:],
-                        start=(g == 0 and half == 1),
-                        stop=(g == GROUPS - 1 and half == 0),
-                    )
-        for u in (4, 5, 6, 7):
-            minus_logits(u, gate[u - 4])
-        for u in (4, 5, 6, 7):
-            weights(u)
-
-        kv_a = [psum.tile([P, 512], F32, tag="bank%d" % j, name="kv_a%d" % j) for j in range(4)]
-        mx_block(KV, 1536, [b[:, 0:256] for b in kv_a])
-        mx_block(KV, 512, [b[:, 256:512] for b in kv_a])
-
-        for u in (0, 1, 2, 3):
-            minus_logits(u, gate[u + 4])
-            weights(u)
+        mx_block(GATE, 1536, [b[:, 0:256] for b in gate_a], every[2:])
+        mx_block(GATE, 512, [b[:, 256:512] for b in gate_a], every)
+        gate_b = [psum.tile([P, 512], F32, tag="bank%d" % (4 + j), name="gate_b%d" % j) for j in range(4)]
+        mx_block(GATE, 1024, [b[:, 0:256] for b in gate_b], every)
+        mx_block(GATE, 0, [b[:, 256:512] for b in gate_b], every)
+        softmax_weights(RNG_A, gate_a)
         nc.vector.reciprocal(out=rden[RNG_A][:], in_=den[RNG_A][:])
 
+        kv_a = [psum.tile([P, 512], F32, tag="bank%d" % j, name="kv_a%d" % j) for j in range(4)]
+        mx_block(KV, 1536, [b[:, 0:256] for b in kv_a], every)
+        mx_block(KV, 512, [b[:, 256:512] for b in kv_a], every)
+
+        softmax_weights(RNG_B, gate_b)
+        nc.vector.reciprocal(out=rden[RNG_B][:], in_=den[RNG_B][:])
+        for j in range(4):
+            e_lo = e_tiles[j][:, 320:544].rearrange("p (k s) -> p k s", s=32)
+            nc.vector.tensor_tensor(
+                out=e_lo,
+                in0=e_lo,
+                in1=rden[RNG_B][:, j, 1:8].unsqueeze(2).to_broadcast([P, 7, 32]),
+                op=ALU.mult,
+            )
+
         kv_bh = [psum.tile([P, 256], F32, tag="bank%d" % (4 + j), name="kv_bh%d" % j) for j in range(4)]
-        mx_block(KV, 1024, [b[:] for b in kv_bh])
+        mx_block(KV, 1024, [b[:] for b in kv_bh], every)
 
         for j in range(4):
             nc.vector.tensor_tensor(
@@ -303,16 +316,6 @@ def tile_deepseekv4csacompressor_w_kernel(
         for j in range(4):
             nc.vector.tensor_reduce(
                 out=num_a[:, j, :], in_=window_view(prod_a[:, j, :]), axis=AX.XY, op=ALU.add
-            )
-            if j == 0:
-                nc.vector.reciprocal(out=rden[RNG_B][:], in_=den[RNG_B][:])
-        for j in range(4):
-            e_lo = e_tiles[j][:, 320:544].rearrange("p (k s) -> p k s", s=32)
-            nc.gpsimd.tensor_tensor(
-                out=e_lo,
-                in0=e_lo,
-                in1=rden[RNG_B][:, j, 1:8].unsqueeze(2).to_broadcast([P, 7, 32]),
-                op=ALU.mult,
             )
         nc.vector.tensor_tensor(
             out=pooled[RNG_A][:, 0:32].rearrange("p (i j) -> p j i", j=4),
@@ -340,10 +343,10 @@ def tile_deepseekv4csacompressor_w_kernel(
         )
 
         kv_bl = [psum.tile([P, 256], F32, tag="bank%d" % j, name="kv_bl%d" % j) for j in range(4)]
-        mx_block(KV, 0, [b[:] for b in kv_bl[0:2]])
+        mx_block(KV, 0, [b[:] for b in kv_bl[0:2]], every)
         fa = psum.tile([P, P], F32, tag="bank4", name="fa")
         nc.tensor.transpose(fa[:], pooled[RNG_A][:], ident_f[:])
-        mx_block(KV, 256, [b[:] for b in kv_bl[2:4]])
+        mx_block(KV, 256, [b[:] for b in kv_bl[2:4]], every)
 
         R = 32
         res_a = const.tile([P, P], F32, name="res_a")

@@ -116,12 +116,13 @@ def tile_deepseekv4csacompressor_w_kernel(
         load_words(GATE, 1536, 512, [[2, 3]])
         load_scales(nc.sync, I32, GATE, 1)
         load_words(GATE, 1536, 512, [[4, 5], [6, 7]])
-        load_scales(nc.gpsimd, F32, KV, 0)
-        load_scales(nc.gpsimd, F32, KV, 1)
         load_words(GATE, 512, 512, pairs)
         load_words(GATE, 1024, 512, pairs)
         load_words(GATE, 0, 512, pairs)
-        load_words(KV, 1536, 512, pairs)
+        load_scales(nc.sync, I32, KV, 0)
+        load_words(KV, 1536, 512, [[0, 1]])
+        load_scales(nc.sync, I32, KV, 1)
+        load_words(KV, 1536, 512, [[2, 3], [4, 5], [6, 7]])
         load_words(KV, 512, 512, pairs)
         load_words(KV, 1024, 512, pairs)
         load_words(KV, 0, 256, [[0, 1, 2, 3], [4, 5, 6, 7]])
@@ -342,11 +343,11 @@ def tile_deepseekv4csacompressor_w_kernel(
             out=pooled_b[:, :, 0], in0=num_b[:, :, 0], in1=rden[RNG_B][:, :, 0], op=ALU.mult
         )
 
-        kv_bl = [psum.tile([P, 256], F32, tag="bank%d" % j, name="kv_bl%d" % j) for j in range(4)]
-        mx_block(KV, 0, [b[:] for b in kv_bl[0:2]], every)
-        fa = psum.tile([P, P], F32, tag="bank4", name="fa")
+        kv_bl = [psum.tile([P, 256], F32, tag="bank%d" % j, name="kv_bl%d" % j) for j in range(2)]
+        mx_block(KV, 0, [b[:] for b in kv_bl], every[:2])
+        fa = psum.tile([P, P], F32, tag="bank3", name="fa")
         nc.tensor.transpose(fa[:], pooled[RNG_A][:], ident_f[:])
-        mx_block(KV, 256, [b[:] for b in kv_bl[2:4]], every)
+        mx_block(KV, 0, [b[:] for b in kv_bl], every[2:])
 
         R = 32
         res_a = const.tile([P, P], F32, name="res_a")
@@ -361,7 +362,10 @@ def tile_deepseekv4csacompressor_w_kernel(
         nc.gpsimd.tensor_tensor(out=t_sin[0:R, :, 1], in0=v[:, :, 0], in1=sin_cos[0:R, 0:32], op=ALU.mult)
         nc.gpsimd.tensor_tensor(out=v[:, :, 0], in0=t_cos[0:R, :, 0], in1=t_sin[0:R, :, 0], op=ALU.subtract)
         nc.gpsimd.tensor_tensor(out=v[:, :, 1], in0=t_cos[0:R, :, 1], in1=t_sin[0:R, :, 1], op=ALU.add)
-        nc.gpsimd.dma_start(out=out_v[1], in_=res_a[0:R, :])
+        nc.sync.dma_start(out=out_v[1], in_=res_a[0:R, :])
+
+        kv_bl.extend([psum.tile([P, 256], F32, tag="bank%d" % j, name="kv_bl%d" % j) for j in (2, 3)])
+        mx_block(KV, 256, [b[:] for b in kv_bl[2:4]], every)
 
         for pair in range(2):
             for j in (2 * pair, 2 * pair + 1):

@@ -25,6 +25,7 @@ TWO_PI_HI = 6.28125
 TWO_PI_LO = 2.0 * math.pi - TWO_PI_HI
 EW = 640
 FAR = 1.0e30
+PAD = 48
 
 
 def store_view(t):
@@ -53,25 +54,13 @@ def tile_deepseekv4csacompressor_w_kernel(
         make_identity(nc, ident_b[:])
         planes = []
         for w in range(2):
-            pl = const.tile([P, 2, 2048], U8, name="planes%d" % w, align_bytes=64)
+            pl = const.tile([P, 2, 2048], U8, name="planes%d" % w, align_bytes=256)
             nc.vector.memset(pl[:].bitcast(I32), 0)
             planes.append(pl)
-        pooled = []
-        for r in range(2):
-            pt = const.tile([P, P], F32, name="pooled%d" % r)
-            nc.gpsimd.memset(pt[:], 0.0)
-            pooled.append(pt)
         freq = const.tile([P, 32], F32, name="freq")
         nc.gpsimd.memset(freq[:, 0:1], 1.0)
         row_i = const.tile([P, 1], I32, name="row_i")
         nc.gpsimd.iota(row_i[:], pattern=[[0, 1]], base=0, channel_multiplier=1)
-        e_tiles = []
-        for u in range(8):
-            e = const.tile([P, EW], F32, name="e%d" % u)
-            nc.gpsimd.memset(e[:, 288:320], FAR)
-            e_tiles.append(e)
-        prod_a = const.tile([P, 4, EW], F32, name="prod_a")
-        nc.gpsimd.memset(prod_a[:, :, 288:320], 0.0)
 
         bias_sb = const.tile([P, 512], BF16, name="bias_sb")
         nc.scalar.dma_start(out=bias_sb[:], in_=position_bias.rearrange("s (h c) -> (s h) c", h=2))
@@ -97,7 +86,10 @@ def tile_deepseekv4csacompressor_w_kernel(
 
         def load_words(w, c0, ncols, group_lists):
             for gs in group_lists:
-                t = wpool.tile([P, len(gs), ncols], U32, name="w%d_%d_%d" % (w, c0, gs[0]), align_bytes=64)
+                padded = wpool.tile(
+                    [P, PAD + len(gs) * ncols], U32, name="w%d_%d_%d" % (w, c0, gs[0]), align_bytes=256
+                )
+                t = padded[:, PAD:].rearrange("p (g n) -> p g n", g=len(gs))
                 nc.sync.dma_start(
                     out=t[:].bitcast(I32),
                     in_=words[w][gs[0] : gs[-1] + 1, :, c0 : c0 + ncols, :]
@@ -113,20 +105,30 @@ def tile_deepseekv4csacompressor_w_kernel(
         load_scales(nc.sync, I32, GATE, 0)
         load_words(GATE, 1536, 512, [[0], [1]])
         load_x(1)
-        load_words(GATE, 1536, 512, [[2, 3]])
-        load_scales(nc.sync, I32, GATE, 1)
-        load_words(GATE, 1536, 512, [[4, 5], [6, 7]])
-        load_words(GATE, 512, 512, pairs)
-        load_words(GATE, 1024, 512, pairs)
+        load_words(GATE, 1536, 512, [[2, 3], [4, 5], [6, 7]])
+        load_scales(nc.gpsimd, F32, GATE, 1)
+        load_scales(nc.gpsimd, F32, KV, 0)
+        load_scales(nc.gpsimd, F32, KV, 1)
+        load_words(GATE, 512, 1024, pairs)
         load_words(GATE, 0, 512, pairs)
-        load_scales(nc.sync, I32, KV, 0)
-        load_words(KV, 1536, 512, [[0, 1]])
-        load_scales(nc.sync, I32, KV, 1)
-        load_words(KV, 1536, 512, [[2, 3], [4, 5], [6, 7]])
+        load_words(KV, 1536, 512, pairs)
         load_words(KV, 512, 512, pairs)
         load_words(KV, 1024, 512, pairs)
         load_words(KV, 0, 256, [[0, 1, 2, 3], [4, 5, 6, 7]])
         load_words(KV, 256, 256, [[0, 1, 2, 3], [4, 5], [6], [7]])
+
+        pooled = []
+        for r in range(2):
+            pt = const.tile([P, P], F32, name="pooled%d" % r)
+            nc.gpsimd.memset(pt[:], 0.0)
+            pooled.append(pt)
+        e_tiles = []
+        for u in range(8):
+            e = const.tile([P, EW], F32, name="e%d" % u)
+            nc.gpsimd.memset(e[:, 288:320], FAR)
+            e_tiles.append(e)
+        prod_a = const.tile([P, 4, EW], F32, name="prod_a")
+        nc.gpsimd.memset(prod_a[:, :, 288:320], 0.0)
 
         bt = psum.tile([P, 4, P], BF16, tag="bank7", name="bt")
         for b in range(4):
@@ -146,8 +148,8 @@ def tile_deepseekv4csacompressor_w_kernel(
         x_scl = []
         for g in range(GROUPS):
             grouped.append(const.tile([P, 4 * TOK], BF16, name="grouped%d" % g, align_bytes=64))
-            x_codes.append(const.tile([P, TOK], U32, name="x_codes%d" % g, align_bytes=64))
-            x_scl.append(const.tile([P, TOK], U8, name="x_scl%d" % g, align_bytes=64))
+            x_codes.append(const.tile([P, TOK], U32, name="x_codes%d" % g, align_bytes=256))
+            x_scl.append(const.tile([P, TOK], U8, name="x_scl%d" % g, align_bytes=256))
 
         def quantise(g):
             nc.vector.quantize_mx(
@@ -281,9 +283,8 @@ def tile_deepseekv4csacompressor_w_kernel(
         out_v = out[0].rearrange("i (h j c) -> h i j c", h=2, j=4)
 
         mx_block(GATE, 1536, [b[:, 0:256] for b in gate_a], every[2:])
-        mx_block(GATE, 512, [b[:, 256:512] for b in gate_a], every)
         gate_b = [psum.tile([P, 512], F32, tag="bank%d" % (4 + j), name="gate_b%d" % j) for j in range(4)]
-        mx_block(GATE, 1024, [b[:, 0:256] for b in gate_b], every)
+        mx_block(GATE, 512, [b[:, 256:512] for b in gate_a] + [b[:, 0:256] for b in gate_b], every)
         mx_block(GATE, 0, [b[:, 256:512] for b in gate_b], every)
         softmax_weights(RNG_A, gate_a)
         nc.vector.reciprocal(out=rden[RNG_A][:], in_=den[RNG_A][:])
@@ -326,7 +327,7 @@ def tile_deepseekv4csacompressor_w_kernel(
         )
 
         num_b = const.tile([P, 4, 8], F32, name="num_b")
-        prod_bh = const.tile([P, 4, 256], F32, name="prod_bh")
+        prod_bh = const.tile([P, 4, 256], F32, name="prod_bh", tag="x_sb0_0")
         for j in range(4):
             nc.vector.tensor_tensor(
                 out=prod_bh[:, j, :], in0=kv_bh[j][:], in1=e_tiles[j][:, 0:256], op=ALU.mult
@@ -334,7 +335,7 @@ def tile_deepseekv4csacompressor_w_kernel(
         nc.vector.tensor_reduce(
             out=num_b[:], in_=prod_bh[:].rearrange("p j (k s) -> p j k s", s=32), axis=AX.X, op=ALU.add
         )
-        prod_bl = const.tile([P, 4, 7, 33], F32, name="prod_bl")
+        prod_bl = const.tile([P, 4, 7, 33], F32, name="prod_bl", tag="x_sb1_0")
         pooled_b = pooled[RNG_B][:, 0:32].rearrange("p (i j) -> p j i", j=4)
         nc.vector.tensor_tensor(
             out=prod_bl[:, :, :, 32], in0=num_b[:, :, 1:8], in1=rden[RNG_B][:, :, 1:8], op=ALU.mult
@@ -343,11 +344,11 @@ def tile_deepseekv4csacompressor_w_kernel(
             out=pooled_b[:, :, 0], in0=num_b[:, :, 0], in1=rden[RNG_B][:, :, 0], op=ALU.mult
         )
 
-        kv_bl = [psum.tile([P, 256], F32, tag="bank%d" % j, name="kv_bl%d" % j) for j in range(2)]
-        mx_block(KV, 0, [b[:] for b in kv_bl], every[:2])
-        fa = psum.tile([P, P], F32, tag="bank3", name="fa")
+        kv_bl = [psum.tile([P, 256], F32, tag="bank%d" % j, name="kv_bl%d" % j) for j in range(4)]
+        mx_block(KV, 0, [b[:] for b in kv_bl[0:2]], every)
+        fa = psum.tile([P, P], F32, tag="bank4", name="fa")
         nc.tensor.transpose(fa[:], pooled[RNG_A][:], ident_f[:])
-        mx_block(KV, 0, [b[:] for b in kv_bl], every[2:])
+        mx_block(KV, 256, [b[:] for b in kv_bl[2:4]], every)
 
         R = 32
         res_a = const.tile([P, P], F32, name="res_a")
@@ -362,10 +363,7 @@ def tile_deepseekv4csacompressor_w_kernel(
         nc.gpsimd.tensor_tensor(out=t_sin[0:R, :, 1], in0=v[:, :, 0], in1=sin_cos[0:R, 0:32], op=ALU.mult)
         nc.gpsimd.tensor_tensor(out=v[:, :, 0], in0=t_cos[0:R, :, 0], in1=t_sin[0:R, :, 0], op=ALU.subtract)
         nc.gpsimd.tensor_tensor(out=v[:, :, 1], in0=t_cos[0:R, :, 1], in1=t_sin[0:R, :, 1], op=ALU.add)
-        nc.sync.dma_start(out=out_v[1], in_=res_a[0:R, :])
-
-        kv_bl.extend([psum.tile([P, 256], F32, tag="bank%d" % j, name="kv_bl%d" % j) for j in (2, 3)])
-        mx_block(KV, 256, [b[:] for b in kv_bl[2:4]], every)
+        nc.gpsimd.dma_start(out=out_v[1], in_=res_a[0:R, :])
 
         for pair in range(2):
             for j in (2 * pair, 2 * pair + 1):

from contextlib import ExitStack
import math

import concourse.mybir as mybir
from concourse.masks import make_identity

F32 = mybir.dt.float32
BF16 = mybir.dt.bfloat16
I32 = mybir.dt.int32
U32 = mybir.dt.uint32
U8 = mybir.dt.uint8
FP8X4 = mybir.dt.float8_e4m3fn_x4
ALU = mybir.AluOpType
ACT = mybir.ActivationFunctionType
AX = mybir.AxisListType

FLOPS = 2 * 256 * 4096 * 4096

P = 128
GROUPS = 8
TOK = 256
GATE, KV = 0, 1
RNG_A, RNG_B = 0, 1
TWO_PI_HI = 6.28125
TWO_PI_LO = 2.0 * math.pi - TWO_PI_HI
EW = 640
FAR = 1.0e30
PAD = 48


def store_view(t):
    return t.rearrange("p (h c) -> p h c", h=2)[:, :, 0:256].rearrange("p h (k s) -> p h k s", s=32)


def window_view(t):
    return t[:, 0:576].rearrange("p (h k s) -> p k h s", h=2, k=9, s=32)[:, 0:8]


def tile_deepseekv4csacompressor_w_kernel(
    tc, hidden_states, w_kv_words, w_kv_scales, w_gate_words, w_gate_scales, position_bias, out
):
    nc = tc.nc
    words = (w_gate_words, w_kv_words)
    scales = (w_gate_scales, w_kv_scales)
    with ExitStack() as ctx:
        const = ctx.enter_context(tc.tile_pool(name="const", bufs=1))
        wpool = ctx.enter_context(tc.tile_pool(name="weights", bufs=1))
        psum = ctx.enter_context(tc.psum_pool(name="psum", bufs=1))
        ctx.enter_context(tc.manual_schedule())

        ident_f = const.tile([P, P], F32, name="ident_f")
        make_identity(nc, ident_f[:])
        ident_b = const.tile([P, P], BF16, name="ident_b")
        make_identity(nc, ident_b[:])
        planes = []
        for w in range(2):
            pl = const.tile([P, 2, 2048], U8, name="planes%d" % w, align_bytes=256)
            nc.vector.memset(pl[:].bitcast(I32), 0)
            planes.append(pl)
        freq = const.tile([P, 32], F32, name="freq")
        nc.gpsimd.memset(freq[:, 0:1], 1.0)
        row_i = const.tile([P, 1], I32, name="row_i")
        nc.gpsimd.iota(row_i[:], pattern=[[0, 1]], base=0, channel_multiplier=1)

        bias_sb = const.tile([P, 512], BF16, name="bias_sb")
        nc.scalar.dma_start(out=bias_sb[:], in_=position_bias.rearrange("s (h c) -> (s h) c", h=2))
        x_sb = {}

        def load_x(half):
            for tt in range(2):
                xs = const.tile([P, 2048], BF16, name="x_sb%d_%d" % (tt, half))
                nc.sync.dma_start(
                    out=xs[:],
                    in_=hidden_states[0, tt * P : (tt + 1) * P, half * 2048 : (half + 1) * 2048],
                )
                x_sb[(tt, half)] = xs

        def load_scales(queue, view, w, a):
            for q in range(4):
                queue.dma_start(
                    out=planes[w][32 * q : 32 * q + 16, a, :].bitcast(view),
                    in_=scales[w][4 * a : 4 * a + 4, 4 * q : 4 * q + 4, :].bitcast(view),
                )

        wt = {}

        def load_words(w, c0, ncols, group_lists):
            for gs in group_lists:
                padded = wpool.tile(
                    [P, PAD + len(gs) * ncols], U32, name="w%d_%d_%d" % (w, c0, gs[0]), align_bytes=256
                )
                t = padded[:, PAD:].rearrange("p (g n) -> p g n", g=len(gs))
                nc.sync.dma_start(
                    out=t[:].bitcast(I32),
                    in_=words[w][gs[0] : gs[-1] + 1, :, c0 : c0 + ncols, :]
                    .rearrange("g p n t -> p g (n t)")
                    .bitcast(I32),
                )
                for k in range(len(gs)):
                    for j in range(ncols // P):
                        wt[(w, c0 + j * P, gs[k])] = t[:, k, j * P : (j + 1) * P]

        pairs = [[0, 1], [2, 3], [4, 5], [6, 7]]
        load_x(0)
        load_scales(nc.sync, I32, GATE, 0)
        load_words(GATE, 1536, 512, [[0], [1]])
        load_x(1)
        load_words(GATE, 1536, 512, [[2, 3], [4, 5], [6, 7]])
        load_scales(nc.gpsimd, F32, GATE, 1)
        load_scales(nc.gpsimd, F32, KV, 0)
        load_scales(nc.gpsimd, F32, KV, 1)
        load_words(GATE, 512, 1024, pairs)
        load_words(GATE, 0, 512, pairs)
        load_words(KV, 1536, 512, pairs)
        load_words(KV, 512, 512, pairs)
        load_words(KV, 1024, 512, pairs)
        load_words(KV, 0, 256, [[0, 1, 2, 3], [4, 5, 6, 7]])
        load_words(KV, 256, 256, [[0, 1, 2, 3], [4, 5], [6], [7]])

        pooled = []
        for r in range(2):
            pt = const.tile([P, P], F32, name="pooled%d" % r)
            nc.gpsimd.memset(pt[:], 0.0)
            pooled.append(pt)
        e_tiles = []
        for u in range(8):
            e = const.tile([P, EW], F32, name="e%d" % u)
            nc.gpsimd.memset(e[:, 288:320], FAR)
            e_tiles.append(e)
        prod_a = const.tile([P, 4, EW], F32, name="prod_a")
        nc.gpsimd.memset(prod_a[:, :, 288:320], 0.0)

        bt = psum.tile([P, 4, P], BF16, tag="bank7", name="bt")
        for b in range(4):
            nc.tensor.transpose(bt[:, b, :], bias_sb[:, b * P : (b + 1) * P], ident_b[:])
        neg_bias = const.tile([P, 8, 64], F32, name="neg_bias")
        bt_v = bt[:].rearrange("p b (s h) -> p h b s", h=2)
        nb_v = neg_bias[:].rearrange("p (h b) s -> p h b s", h=2)
        nc.vector.tensor_scalar(
            out=nb_v[:, :, :, 0:32], in0=bt_v[:, :, :, 32:64], scalar1=-1.0, scalar2=None, op0=ALU.mult
        )
        nc.vector.tensor_scalar(
            out=nb_v[:, :, :, 32:64], in0=bt_v[:, :, :, 0:32], scalar1=-1.0, scalar2=None, op0=ALU.mult
        )

        grouped = []
        x_codes = []
        x_scl = []
        for g in range(GROUPS):
            grouped.append(const.tile([P, 4 * TOK], BF16, name="grouped%d" % g, align_bytes=64))
            x_codes.append(const.tile([P, TOK], U32, name="x_codes%d" % g, align_bytes=256))
            x_scl.append(const.tile([P, TOK], U8, name="x_scl%d" % g, align_bytes=256))

        def quantise(g):
            nc.vector.quantize_mx(
                out=x_codes[g][:].bitcast(FP8X4), scales=x_scl[g][:], in_=grouped[g][:]
            )

        def prepare_x(half):
            for g in range(4 * half, 4 * half + 4):
                xt = psum.tile([P, 2, TOK], F32, tag="bank%d" % (4 + g % 4), name="xt%d" % g)
                for tt in range(2):
                    src = x_sb[(tt, half)][:].bitcast(F32)
                    for u in range(2):
                        w0 = 256 * (g % 4)
                        nc.tensor.transpose(
                            xt[:, u, tt * P : (tt + 1) * P], src[:, w0 + u : w0 + 256 : 2], ident_f[:]
                        )
                dst = grouped[g][:].bitcast(F32).rearrange("p (t u) -> p t u", u=2)
                if g % 4 == 3:
                    nc.vector.tensor_copy(out=dst, in_=xt[:].rearrange("p u t -> p t u"))
                else:
                    nc.scalar.copy(out=dst, in_=xt[:].rearrange("p u t -> p t u"))
                if g % 4 >= 1:
                    quantise(g - 1)
            quantise(4 * half + 3)

        def mx_block(w, c0, outs, groups):
            for g in groups:
                for j in range(len(outs)):
                    c = c0 + j * P
                    nc.tensor.matmul_mx(
                        out=outs[j],
                        lhsT=wt[(w, c, g)].bitcast(FP8X4),
                        lhsT_scale=planes[w][4 * (g % 4) : P, g // 4, c : c + P],
                        rhs=x_codes[g][:].bitcast(FP8X4),
                        rhs_scale=x_scl[g][:],
                        start=(g == 0),
                        stop=(g == GROUPS - 1),
                    )

        every = list(range(GROUPS))
        prepare_x(0)
        gate_a = [psum.tile([P, 512], F32, tag="bank%d" % j, name="gate_a%d" % j) for j in range(4)]
        mx_block(GATE, 1536, [b[:, 0:256] for b in gate_a], [0, 1])
        prepare_x(1)

        win_i = const.tile([P, 1], I32, name="win_i")
        nc.vector.tensor_scalar(
            out=win_i[:], in0=row_i[:], scalar1=2, scalar2=7, op0=ALU.logical_shift_right, op1=ALU.bitwise_and
        )
        unit_i = const.tile([P, 1], I32, name="unit_i")
        nc.vector.tensor_single_scalar(out=unit_i[:], in_=row_i[:], scalar=3, op=ALU.bitwise_and)
        win_f = const.tile([P, 1], F32, name="win_f")
        nc.vector.tensor_copy(out=win_f[:], in_=win_i[:])
        unit_f = const.tile([P, 1], F32, name="unit_f")
        nc.vector.tensor_copy(out=unit_f[:], in_=unit_i[:])
        step_f = const.tile([P, 1], F32, name="step_f")
        nc.vector.tensor_scalar(
            out=step_f[:], in0=unit_f[:], scalar1=3.0, scalar2=32.0, op0=ALU.is_equal, op1=ALU.mult
        )
        for b in range(5):
            n = 2 ** b
            nc.vector.tensor_scalar(
                out=freq[:, n : 2 * n],
                in0=freq[:, 0:n],
                scalar1=10000.0 ** (-2.0 * n / 64.0),
                scalar2=None,
                op0=ALU.mult,
            )
        pos_f = const.tile([P, 1], F32, name="pos_f")
        nc.vector.tensor_tensor(out=pos_f[:], in0=win_f[:], in1=step_f[:], op=ALU.mult)
        angle = const.tile([P, 64], F32, name="angle")
        nc.vector.tensor_scalar(
            out=angle[:, 0:32], in0=freq[:], scalar1=pos_f[:, 0:1], scalar2=None, op0=ALU.mult
        )
        nc.vector.tensor_scalar(
            out=angle[:, 32:64], in0=angle[:, 0:32], scalar1=0.5 * math.pi, scalar2=None, op0=ALU.add
        )
        turns_i = const.tile([P, 64], I32, name="turns_i")
        nc.vector.tensor_scalar(
            out=turns_i[:], in0=angle[:], scalar1=0.5 / math.pi, scalar2=None, op0=ALU.mult
        )
        turns_f = const.tile([P, 64], F32, name="turns_f")
        nc.vector.tensor_copy(out=turns_f[:], in_=turns_i[:])
        red = const.tile([P, 64], F32, name="red")
        nc.vector.scalar_tensor_tensor(
            out=red[:], in0=turns_f[:], scalar=-TWO_PI_HI, in1=angle[:], op0=ALU.mult, op1=ALU.add
        )
        nc.vector.scalar_tensor_tensor(
            out=red[:], in0=turns_f[:], scalar=-TWO_PI_LO, in1=red[:], op0=ALU.mult, op1=ALU.add
        )
        fold = const.tile([P, 64], F32, name="fold")
        nc.vector.tensor_scalar(
            out=fold[:], in0=red[:], scalar1=math.pi, scalar2=-2.0 * math.pi, op0=ALU.is_gt, op1=ALU.mult
        )
        nc.vector.tensor_tensor(out=red[:], in0=red[:], in1=fold[:], op=ALU.add)
        sin_cos = const.tile([P, 64], F32, name="sin_cos")
        nc.scalar.activation(out=sin_cos[:], in_=red[:], func=ACT.Sin)
        warm = const.tile([P, 1], F32, name="warm")
        nc.scalar.activation(out=warm[:], in_=sin_cos[:, 0:1], func=ACT.Exp)

        neg_max = [const.tile([P, 4, 8], F32, name="neg_max%d" % r) for r in range(2)]
        den = [const.tile([P, 4, 8], F32, name="den%d" % r) for r in range(2)]
        rden = [const.tile([P, 4, 8], F32, name="rden%d" % r) for r in range(2)]

        def softmax_weights(rng, banks):
            for j in range(4):
                u = j + (4 if rng == RNG_A else 0)
                e = e_tiles[u]
                nc.vector.tensor_tensor(
                    out=store_view(e[:]),
                    in0=neg_bias[:, u, :]
                    .rearrange("p (h s) -> p h s", h=2)
                    .unsqueeze(2)
                    .to_broadcast([P, 2, 8, 32]),
                    in1=banks[j][:].rearrange("p (h k s) -> p h k s", h=2, k=8),
                    op=ALU.subtract,
                )
                nc.vector.tensor_reduce(
                    out=neg_max[rng][:, j, :], in_=window_view(e[:]), axis=AX.XY, op=ALU.min
                )
                for i in range(8):
                    nc.scalar.activation(
                        out=window_view(e[:])[:, i],
                        in_=window_view(e[:])[:, i],
                        func=ACT.Exp,
                        bias=neg_max[rng][:, j, i : i + 1],
                        scale=-1.0,
                        accum_out=den[rng][:, j, i : i + 1],
                    )

        out_v = out[0].rearrange("i (h j c) -> h i j c", h=2, j=4)

        mx_block(GATE, 1536, [b[:, 0:256] for b in gate_a], every[2:])
        gate_b = [psum.tile([P, 512], F32, tag="bank%d" % (4 + j), name="gate_b%d" % j) for j in range(4)]
        mx_block(GATE, 512, [b[:, 256:512] for b in gate_a] + [b[:, 0:256] for b in gate_b], every)
        mx_block(GATE, 0, [b[:, 256:512] for b in gate_b], every)
        softmax_weights(RNG_A, gate_a)
        nc.vector.reciprocal(out=rden[RNG_A][:], in_=den[RNG_A][:])

        kv_a = [psum.tile([P, 512], F32, tag="bank%d" % j, name="kv_a%d" % j) for j in range(4)]
        mx_block(KV, 1536, [b[:, 0:256] for b in kv_a], every)
        mx_block(KV, 512, [b[:, 256:512] for b in kv_a], every)

        softmax_weights(RNG_B, gate_b)
        nc.vector.reciprocal(out=rden[RNG_B][:], in_=den[RNG_B][:])
        for j in range(4):
            e_lo = e_tiles[j][:, 320:544].rearrange("p (k s) -> p k s", s=32)
            nc.vector.tensor_tensor(
                out=e_lo,
                in0=e_lo,
                in1=rden[RNG_B][:, j, 1:8].unsqueeze(2).to_broadcast([P, 7, 32]),
                op=ALU.mult,
            )

        kv_bh = [psum.tile([P, 256], F32, tag="bank%d" % (4 + j), name="kv_bh%d" % j) for j in range(4)]
        mx_block(KV, 1024, [b[:] for b in kv_bh], every)

        for j in range(4):
            nc.vector.tensor_tensor(
                out=store_view(prod_a[:, j, :]),
                in0=kv_a[j][:].rearrange("p (h k s) -> p h k s", h=2, k=8),
                in1=store_view(e_tiles[4 + j][:]),
                op=ALU.mult,
            )
        num_a = const.tile([P, 4, 8], F32, name="num_a")
        for j in range(4):
            nc.vector.tensor_reduce(
                out=num_a[:, j, :], in_=window_view(prod_a[:, j, :]), axis=AX.XY, op=ALU.add
            )
        nc.vector.tensor_tensor(
            out=pooled[RNG_A][:, 0:32].rearrange("p (i j) -> p j i", j=4),
            in0=num_a[:],
            in1=rden[RNG_A][:],
            op=ALU.mult,
        )

        num_b = const.tile([P, 4, 8], F32, name="num_b")
        prod_bh = const.tile([P, 4, 256], F32, name="prod_bh", tag="x_sb0_0")
        for j in range(4):
            nc.vector.tensor_tensor(
                out=prod_bh[:, j, :], in0=kv_bh[j][:], in1=e_tiles[j][:, 0:256], op=ALU.mult
            )
        nc.vector.tensor_reduce(
            out=num_b[:], in_=prod_bh[:].rearrange("p j (k s) -> p j k s", s=32), axis=AX.X, op=ALU.add
        )
        prod_bl = const.tile([P, 4, 7, 33], F32, name="prod_bl", tag="x_sb1_0")
        pooled_b = pooled[RNG_B][:, 0:32].rearrange("p (i j) -> p j i", j=4)
        nc.vector.tensor_tensor(
            out=prod_bl[:, :, :, 32], in0=num_b[:, :, 1:8], in1=rden[RNG_B][:, :, 1:8], op=ALU.mult
        )
        nc.vector.tensor_tensor(
            out=pooled_b[:, :, 0], in0=num_b[:, :, 0], in1=rden[RNG_B][:, :, 0], op=ALU.mult
        )

        kv_bl = [psum.tile([P, 256], F32, tag="bank%d" % j, name="kv_bl%d" % j) for j in range(4)]
        mx_block(KV, 0, [b[:] for b in kv_bl[0:2]], every)
        fa = psum.tile([P, P], F32, tag="bank4", name="fa")
        nc.tensor.transpose(fa[:], pooled[RNG_A][:], ident_f[:])
        mx_block(KV, 256, [b[:] for b in kv_bl[2:4]], every)

        R = 32
        res_a = const.tile([P, P], F32, name="res_a")
        t_cos = const.tile([P, 32, 2], F32, name="t_cos")
        t_sin = const.tile([P, 32, 2], F32, name="t_sin")
        nc.scalar.copy(out=res_a[0:R, :], in_=fa[0:R, :])
        v = res_a[0:R, 64:128].rearrange("p (j e) -> p j e", e=2)
        nc.gpsimd.tensor_tensor(
            out=t_cos[0:R], in0=v, in1=sin_cos[0:R, 32:64].unsqueeze(2).to_broadcast([R, 32, 2]), op=ALU.mult
        )
        nc.gpsimd.tensor_tensor(out=t_sin[0:R, :, 0], in0=v[:, :, 1], in1=sin_cos[0:R, 0:32], op=ALU.mult)
        nc.gpsimd.tensor_tensor(out=t_sin[0:R, :, 1], in0=v[:, :, 0], in1=sin_cos[0:R, 0:32], op=ALU.mult)
        nc.gpsimd.tensor_tensor(out=v[:, :, 0], in0=t_cos[0:R, :, 0], in1=t_sin[0:R, :, 0], op=ALU.subtract)
        nc.gpsimd.tensor_tensor(out=v[:, :, 1], in0=t_cos[0:R, :, 1], in1=t_sin[0:R, :, 1], op=ALU.add)
        nc.gpsimd.dma_start(out=out_v[1], in_=res_a[0:R, :])

        for pair in range(2):
            for j in (2 * pair, 2 * pair + 1):
                nc.vector.tensor_tensor(
                    out=prod_bl[:, j, :, 0:32],
                    in0=kv_bl[j][:, 0:224].rearrange("p (k s) -> p k s", s=32),
                    in1=e_tiles[j][:, 320:544].rearrange("p (k s) -> p k s", s=32),
                    op=ALU.mult,
                )
            nc.vector.tensor_reduce(
                out=pooled_b[:, 2 * pair : 2 * pair + 2, 1:8],
                in_=prod_bl[:, 2 * pair : 2 * pair + 2],
                axis=AX.X,
                op=ALU.add,
            )
        fb = psum.tile([P, P], F32, tag="bank5", name="fb")
        nc.tensor.transpose(fb[:], pooled[RNG_B][:], ident_f[:])
        res_b = const.tile([P, P], F32, name="res_b")
        nc.vector.tensor_copy(out=res_b[0:R, :], in_=fb[0:R, :])
        nc.sync.dma_start(out=out_v[0], in_=res_b[0:R, :])
